import numpy as np
import ml_dtypes


def mxq(x, axis, fmt="e4m3"):
    dtype, down = {"e4m3": (ml_dtypes.float8_e4m3fn, 7), "e5m2": (ml_dtypes.float8_e5m2, 14)}[fmt]
    v = np.moveaxis(np.asarray(x, np.float32).astype(ml_dtypes.bfloat16).astype(np.float64), axis, -1)
    blocks = v.reshape(v.shape[:-1] + (-1, 32))
    amax = np.abs(blocks).max(-1, keepdims=True)
    byte = np.maximum(np.where(amax > 0, np.frexp(amax)[1] - 1 + 127, 0) - down, 1)
    scale = np.exp2(byte - 127.0)
    codes = (blocks / scale).astype(np.float32).astype(dtype).astype(np.float64)
    return np.moveaxis((codes * scale).reshape(v.shape), -1, axis)


WIDE = False


def mx_kscale(k):
    if not WIDE:
        return np.ones(k)
    levels = np.array([10, -10, 5, -5, 0])
    if k % 512:
        return np.exp2(np.random.permutation(np.resize(levels, k // 32))).repeat(32)
    a = np.empty((k // 512, 16))
    for p in range(k // 512):
        a[p, :8] = np.random.permutation(np.resize(levels, 8))
        for g in range(8):
            far = levels[np.abs(levels - a[p, g]) >= 10]
            a[p, g + 8] = far[np.random.randint(len(far))]
    return np.exp2(a.ravel()).repeat(32)


BF16 = ml_dtypes.bfloat16


def bf(x):
    return np.asarray(x, np.float32).astype(BF16)


def f64(x):
    return np.asarray(x).astype(np.float64)


B, N, C = 16, 16, 1024
NEG_SLOPE = 0.2


def leaky(v):
    return np.where(v >= 0, v, NEG_SLOPE * v)


def setup_inputs():
    s, t = mx_kscale(C), mx_kscale(C)
    w1 = np.random.standard_normal((2, C, C)) * 0.7 / np.sqrt(C) / s[None, :, None] * t
    return {"F": bf(np.random.standard_normal((B, N, C)) * s),
            "W1": bf(w1.reshape(2 * C, C)),
            "b1": bf(np.random.standard_normal(C) * 0.2 * t),
            "W2": bf(np.random.standard_normal((C, C)) / np.sqrt(C) / t[:, None]),
            "b2": bf(np.random.standard_normal(C) * 0.2)}


def reference(F, W1, b1, W2, b2):
    Fq = mxq(f64(F), 2, "e4m3")
    W1 = f64(W1)
    A = Fq @ mxq(W1[:C], 0, "e4m3")
    Bp = Fq @ mxq(W1[C:], 0, "e4m3")
    h = leaky(A[:, :, None, :] + Bp[:, None, :, :] + f64(b1))
    h = leaky((mxq(h, 3, "e4m3") @ mxq(f64(W2), 0, "e4m3")) + f64(b2))
    return h.sum(-2)

@@ -1,0 +1,364 @@
+from contextlib import ExitStack
+
+import concourse.bass as bass
+import concourse.mybir as mybir
+import concourse.tile as tile
+from concourse.masks import make_identity
+
+F32 = mybir.dt.float32
+BF16 = mybir.dt.bfloat16
+U32 = mybir.dt.uint32
+U8 = mybir.dt.uint8
+FP8X4 = mybir.dt.float8_e4m3fn_x4
+ALU = mybir.AluOpType
+ACT = mybir.ActivationFunctionType
+
+P = 128
+C = 1024
+ROWS = 256
+NODES = 16
+SETS = 16
+UNITS = 8
+SLOPE = 0.2
+FLOPS = 2 * ROWS * C * 2 * C + 2 * ROWS * NODES * C * C
+
+
+SEQ = [(n, g) for n in range(NODES) for g in range(2)]
+VSHARE = 84
+V_COMBINE = [13, 14, 15]
+LAG = 2
+
+
+def tile_nonlocalmp_pa_kernel(tc, F, W1, b1, W2, b2, out):
+    nc = tc.nc
+    f_flat = F.flatten_outer_dims()
+    out_flat = out.flatten_outer_dims()
+
+    with ExitStack() as ctx:
+        const = ctx.enter_context(tc.tile_pool(name="const", bufs=1))
+        rawp = ctx.enter_context(tc.tile_pool(name="rawp", bufs=8))
+        grpp = ctx.enter_context(tc.tile_pool(name="grpp", bufs=4))
+        up = ctx.enter_context(tc.tile_pool(name="up", bufs=2))
+        hbp = ctx.enter_context(tc.tile_pool(name="hbp", bufs=3))
+        rlp = ctx.enter_context(tc.tile_pool(name="rlp", bufs=10))
+        resp = ctx.enter_context(tc.tile_pool(name="resp", bufs=4))
+        work = ctx.enter_context(tc.psum_pool(name="work", bufs=4))
+        sump = ctx.enter_context(tc.psum_pool(name="sump", bufs=1))
+        ctx.enter_context(tc.manual_schedule())
+
+        ident32 = const.tile([P, P], F32, name="ident32")
+        make_identity(nc, ident32[:])
+        identb = const.tile([P, P], BF16, name="identb")
+        make_identity(nc, identb[:])
+        bt = const.tile([P, P], BF16, name="bt")
+        nc.vector.memset(bt[:], 0.0)
+
+        fsb = const.tile([P, 2, C], BF16, name="fsb")
+        fg = const.tile([P, 2, ROWS, 4], BF16, name="fg", align_bytes=64)
+        fc = const.tile([P, 2, ROWS], U32, name="fc", align_bytes=64)
+        fs = const.tile([P, 2, ROWS], U8, name="fs", align_bytes=64)
+        w1c = const.tile([P, 2, 2, 2, 512], U32, name="w1c", align_bytes=64)
+        w1s = const.tile([P, 2, 2, 2, 512], U8, name="w1s", align_bytes=64)
+        w2c = const.tile([P, 2, C], U32, name="w2c", align_bytes=64)
+        w2s = const.tile([P, 2, C], U8, name="w2s", align_bytes=64)
+        hc = const.tile([P, NODES, 2, ROWS], U32, name="hc", align_bytes=64)
+        hs = const.tile([P, NODES, 2, ROWS], U8, name="hs", align_bytes=64)
+        a4 = const.tile([P, 2, ROWS, 4], F32, name="a4")
+        b4 = const.tile([P, 2, ROWS, 4], F32, name="b4")
+        b1c = const.tile([P, 2, 4], BF16, name="b1c")
+        b2r = const.tile([P, 8], F32, name="b2r")
+        b2row = const.tile([P, C], BF16, name="b2row")
+
+        nc.sync.dma_start(out=bt[0:8, :], in_=b2.rearrange("(r c) -> r c", c=P))
+        nc.sync.dma_start(out=b1c[:], in_=b1.rearrange("(g p t) -> p g t", g=2, t=4))
+        nc.sync.dma_start(out=fsb[:], in_=f_flat.rearrange("(f p) c -> p f c", p=P))
+        w1raw = {}
+        w2raw = {}
+        for g in range(2):
+            for ab in range(2):
+                for kp in range(2):
+                    raw = rawp.tile([P, 4, 512], BF16, name="raw")
+                    r0 = ab * C + kp * 512
+                    nc.sync.dma_start(
+                        out=raw[:],
+                        in_=W1[r0 : r0 + 512, g * 512 : (g + 1) * 512].rearrange("(p j) w -> p j w", j=4),
+                    )
+                    w1raw[(g, ab, kp)] = raw
+        for ch in range(2):
+            for g in range(2):
+                raw = rawp.tile([P, 4, 512], BF16, name="raw")
+                nc.sync.dma_start(
+                    out=raw[:],
+                    in_=W2[g * 512 : (g + 1) * 512, ch * 512 : (ch + 1) * 512].rearrange("(p j) n -> p j n", j=4),
+                )
+                w2raw[(g, ch)] = raw
+        nc.sync.dma_start(out=b2row[:], in_=b2.partition_broadcast(P))
+
+        def regroup(raw, vshare):
+            gq = grpp.tile([P, 512, 4], BF16, name="gq", align_bytes=64)
+            dst = gq[:].rearrange("p (c i) t -> p c t i", i=4)
+            src = raw[:].rearrange("p t (c i) -> p c t i", i=4)
+            if vshare > 0:
+                nc.vector.tensor_copy(out=dst[:, 0:vshare], in_=src[:, 0:vshare])
+            if vshare < 128:
+                nc.scalar.copy(out=dst[:, vshare:128], in_=src[:, vshare:128])
+            return gq
+
+        def regroup_w1(raw, vshare):
+            gq = grpp.tile([P, 512, 4], BF16, name="gq", align_bytes=64)
+            dst = gq[:].rearrange("p (t m) j -> p t m j", t=4)
+            src = raw[:].rearrange("p j (m t) -> p t m j", t=4)
+            if vshare > 0:
+                nc.vector.tensor_copy(out=dst[:, :, 0:vshare], in_=src[:, :, 0:vshare])
+            if vshare < 128:
+                nc.scalar.copy(out=dst[:, :, vshare:128], in_=src[:, :, vshare:128])
+            return gq
+
+        def quant(gq, codes, scales):
+            nc.vector.quantize_mx(
+                out=codes.bitcast(FP8X4), scales=scales, in_=gq[:].rearrange("p w t -> p (w t)")
+            )
+
+        btp = work.tile([P, P], BF16, name="wk")
+        nc.tensor.transpose(btp[:], bt[:], identb[:])
+        nc.vector.tensor_scalar_mul(out=b2r[:], in0=btp[:, 0:8], scalar1=1.0 - SLOPE)
+
+        fsb32 = fsb[:].bitcast(F32)
+        fg32 = fg[:].bitcast(F32)
+        for kp in range(2):
+            xt = work.tile([P, 2, ROWS], F32, name="wk")
+            for f in range(2):
+                for u in range(2):
+                    nc.tensor.transpose(
+                        xt[:, u, f * P : (f + 1) * P],
+                        fsb32[:, f, kp * 256 + u : (kp + 1) * 256 : 2],
+                        ident32[:],
+                    )
+            nc.scalar.copy(out=fg32[:, kp], in_=xt[:].rearrange("p u c -> p c u"))
+        nc.vector.quantize_mx(
+            out=fc[:].rearrange("p k c -> p (k c)").bitcast(FP8X4),
+            scales=fs[:].rearrange("p k c -> p (k c)"),
+            in_=fg[:].rearrange("p k c t -> p (k c t)"),
+        )
+
+        def stage1_pe(g, ab, tiles):
+            if True:
+                for f in range(2):
+                    ps = work.tile([P, 4, P], F32, name="wk")
+                    for t in range(4):
+                        for kp in range(2):
+                            nc.tensor.matmul_mx(
+                                out=ps[:, t, :],
+                                lhsT=w1c[:, g, ab, kp, t * P : (t + 1) * P].bitcast(FP8X4),
+                                lhsT_scale=w1s[:, g, ab, kp, t * P : (t + 1) * P],
+                                rhs=fc[:, kp, f * P : (f + 1) * P].bitcast(FP8X4),
+                                rhs_scale=fs[:, kp, f * P : (f + 1) * P],
+                                start=(kp == 0),
+                                stop=(kp == 1),
+                            )
+                    tiles[(ab, f)] = ps
+
+        def evac_a(g, tiles):
+            for f in range(2):
+                nc.vector.tensor_tensor(
+                    out=a4[:, g, f * P : (f + 1) * P, :],
+                    in0=tiles[(0, f)][:].rearrange("p t r -> p r t"),
+                    in1=b1c[:, g, :].unsqueeze(1).to_broadcast([P, P, 4]),
+                    op=ALU.add,
+                )
+
+        def evac_b(g, tiles, second_on_vector):
+            nc.scalar.copy(out=b4[:, g, 0:P, :], in_=tiles[(1, 0)][:].rearrange("p t r -> p r t"))
+            if second_on_vector:
+                nc.vector.tensor_copy(out=b4[:, g, P:ROWS, :], in_=tiles[(1, 1)][:].rearrange("p t r -> p r t"))
+            else:
+                nc.scalar.copy(out=b4[:, g, P:ROWS, :], in_=tiles[(1, 1)][:].rearrange("p t r -> p r t"))
+
+        def w1q(g, idx, gq):
+            quant(gq, w1c[:, g, idx // 2, idx % 2, :], w1s[:, g, idx // 2, idx % 2, :])
+
+        st0 = {}
+        prev = None
+        for idx in range(4):
+            gq = regroup_w1(w1raw[(0, idx // 2, idx % 2)], VSHARE)
+            if prev is not None:
+                w1q(0, prev[1], prev[0])
+                if prev[1] == 1:
+                    stage1_pe(0, 0, st0)
+            prev = (gq, idx)
+        w1q(0, 3, prev[0])
+        stage1_pe(0, 1, st0)
+
+        total = {}
+        for hb in range(2):
+            for ch in range(2):
+                total[(hb, ch)] = sump.tile([P, 512], F32, name="tot%d%d" % (hb, ch))
+        state = {"pending": None, "evac1": False, "w2": 0, "last_e": None, "ready": []}
+        tcount = {}
+        utile = {}
+        hbt = {}
+        rlt = {}
+        ytile = {}
+        done_g = {}
+
+        def main_and_leaky(n):
+            for k in range(4):
+                y = work.tile([P, 2, ROWS], F32, name="wk")
+                for mloc in range(2):
+                    m = 2 * k + mloc
+                    for g in range(2):
+                        nc.tensor.matmul_mx(
+                            out=y[:, mloc, :],
+                            lhsT=w2c[:, g, m * P : (m + 1) * P].bitcast(FP8X4),
+                            lhsT_scale=w2s[:, g, m * P : (m + 1) * P],
+                            rhs=hc[:, n, g, :].bitcast(FP8X4),
+                            rhs_scale=hs[:, n, g, :],
+                            start=(g == 0),
+                            stop=(g == 1),
+                        )
+                rl = rlp.tile([P, 2, 2, ROWS], F32, name="rl")
+                for mloc in range(2):
+                    m = 2 * k + mloc
+                    nc.scalar.activation(
+                        out=rl[:, 0, mloc, :], in_=y[:, mloc, :], func=ACT.Relu, bias=b2r[:, m : m + 1], scale=1.0 - SLOPE
+                    )
+                if n not in V_COMBINE:
+                    nc.scalar.mul(out=rl[:, 1], in_=y[:], mul=SLOPE)
+                rlt[(n, k)] = rl
+                ytile[(n, k)] = y
+
+        def combine(n):
+            if n in V_COMBINE:
+                for k in range(4):
+                    rl = rlt[(n, k)]
+                    nc.vector.scalar_tensor_tensor(
+                        out=rl[:, 1], in0=ytile[(n, k)][:], scalar=SLOPE, in1=rl[:, 0], op0=ALU.mult, op1=ALU.add
+                    )
+
+        def sum_transposes(n):
+            for hb in range(2):
+                for m in range(8):
+                    ch, mm = m // 4, m % 4
+                    for term in ([1] if n in V_COMBINE else [0, 1]):
+                        cnt = tcount.get((hb, ch), 0)
+                        tcount[(hb, ch)] = cnt + 1
+                        nc.tensor.matmul(
+                            out=total[(hb, ch)][:, mm * P : (mm + 1) * P],
+                            lhsT=rlt[(n, m // 2)][:, term, m % 2, hb * P : (hb + 1) * P],
+                            rhs=ident32[:],
+                            is_transpose=True,
+                            start=(cnt == 0),
+                            stop=(cnt == 4 * (2 * NODES - len(V_COMBINE)) - 1),
+                        )
+
+        def stage2(n):
+            assert state["w2"] == 4
+            if state["last_e"] is not None:
+                combine(state["last_e"])
+            main_and_leaky(n)
+            if state["last_e"] is not None:
+                sum_transposes(state["last_e"])
+            state["last_e"] = n
+
+        def flush():
+            q = state["pending"]
+            if q is None:
+                return
+            state["pending"] = None
+            n, g = SEQ[q]
+            nc.vector.quantize_mx(
+                out=hc[:, n, g, :].bitcast(FP8X4), scales=hs[:, n, g, :], in_=hbt[q][:]
+            )
+            done_g[n] = done_g.get(n, 0) + 1
+            if done_g[n] == 2:
+                state["ready"] = state["ready"] + [(n, q)]
+
+        def emit_ready(q_now):
+            while state["ready"] and state["ready"][0][1] + LAG <= q_now:
+                stage2(state["ready"][0][0])
+                state["ready"] = state["ready"][1:]
+
+        def h_add(q):
+            n, g = SEQ[q]
+            assert g == 0 or state["evac1"]
+            u = up.tile([P, SETS, NODES, 4], F32, name="u")
+            utile[q] = u
+            a_view = a4[:, g].rearrange("p (b i) t -> p b i t", i=NODES)
+            b_view = b4[:, g].rearrange("p (b j) t -> p b j t", j=NODES)
+            nc.vector.tensor_tensor(
+                out=u[:],
+                in0=a_view,
+                in1=b_view[:, :, n, :].unsqueeze(2).to_broadcast([P, SETS, NODES, 4]),
+                op=ALU.add,
+            )
+            flush()
+
+        def h_leaky(q):
+            uf = utile[q][:].rearrange("p b i t -> p (b i t)")
+            hb16 = hbp.tile([P, 4 * ROWS], BF16, name="hb16", align_bytes=64)
+            nc.vector.scalar_tensor_tensor(
+                out=hb16[:], in0=uf, scalar=SLOPE, in1=uf, op0=ALU.mult, op1=ALU.max
+            )
+            hbt[q] = hb16
+            state["pending"] = q
+
+        W2ORDER = [(0, 0), (1, 0), (0, 1), (1, 1)]
+
+        def qw2(idx, gq):
+            gg, ch = W2ORDER[idx]
+            quant(gq, w2c[:, gg, ch * 512 : (ch + 1) * 512], w2s[:, gg, ch * 512 : (ch + 1) * 512])
+            state["w2"] = state["w2"] + 1
+
+        st1 = {}
+        g10 = regroup_w1(w1raw[(1, 0, 0)], 0)
+        evac_a(0, st0)
+        evac_b(0, st0, False)
+        g11 = regroup_w1(w1raw[(1, 0, 1)], 128)
+        g12 = regroup_w1(w1raw[(1, 1, 0)], 0)
+        w1q(1, 0, g10)
+        w1q(1, 1, g11)
+        stage1_pe(1, 0, st1)
+        h_add(0)
+        g13 = regroup_w1(w1raw[(1, 1, 1)], 128)
+        w2a = regroup(w2raw[W2ORDER[0]], 0)
+        w2b = regroup(w2raw[W2ORDER[1]], 0)
+        w1q(1, 2, g12)
+        w1q(1, 3, g13)
+        stage1_pe(1, 1, st1)
+        h_leaky(0)
+        evac_b(1, st1, False)
+        evac_a(1, st1)
+        state["evac1"] = True
+        flush()
+        w2c_ = regroup(w2raw[W2ORDER[2]], 0)
+        w2d_ = regroup(w2raw[W2ORDER[3]], 0)
+        h_add(1)
+        qw2(0, w2a)
+        qw2(1, w2b)
+        h_leaky(1)
+        qw2(2, w2c_)
+        flush()
+        qw2(3, w2d_)
+        for q in range(2, len(SEQ)):
+            h_add(q)
+            emit_ready(q)
+            h_leaky(q)
+        flush()
+        emit_ready(len(SEQ) + LAG)
+        combine(state["last_e"])
+        sum_transposes(state["last_e"])
+
+        for ch in range(2):
+            for hb in range(2):
+                res = resp.tile([P, 512], F32, name="res")
+                nc.vector.scalar_tensor_tensor(
+                    out=res[:],
+                    in0=b2row[:, ch * 512 : (ch + 1) * 512],
+                    scalar=SLOPE * NODES,
+                    in1=total[(hb, ch)][:],
+                    op0=ALU.mult,
+                    op1=ALU.add,
+                )
+                nc.sync.dma_start(
+                    out=out_flat[hb * P : (hb + 1) * P, ch * 512 : (ch + 1) * 512], in_=res[:]
+                )

@@ -17,16 +17,17 @@ P = 128
 C = 1024
 ROWS = 256
 NODES = 16
-SETS = 16
-UNITS = 8
+HSETS = 8
+UNITS = 16
 SLOPE = 0.2
 FLOPS = 2 * ROWS * C * 2 * C + 2 * ROWS * NODES * C * C
 
-
-SEQ = [(n, g) for n in range(NODES) for g in range(2)]
+SEQ = [(n, g) for n in range(UNITS) for g in range(2)]
 VSHARE = 84
-V_COMBINE = [13, 14, 15]
-LAG = 2
+V_COMBINE = [11, 12, 13, 14, 15]
+QA = 12
+HELD = min(V_COMBINE) - 1
+G_TILES = [6, 9, 12, 15, 18, 21, 24, 27, 30]
 
 
 def tile_nonlocalmp_pa_kernel(tc, F, W1, b1, W2, b2, out):
@@ -38,13 +39,23 @@ def tile_nonlocalmp_pa_kernel(tc, F, W1, b1, W2, b2, out):
         const = ctx.enter_context(tc.tile_pool(name="const", bufs=1))
         rawp = ctx.enter_context(tc.tile_pool(name="rawp", bufs=8))
         grpp = ctx.enter_context(tc.tile_pool(name="grpp", bufs=4))
-        up = ctx.enter_context(tc.tile_pool(name="up", bufs=2))
-        hbp = ctx.enter_context(tc.tile_pool(name="hbp", bufs=3))
+        up = ctx.enter_context(tc.tile_pool(name="up", bufs=1))
+        hbp = ctx.enter_context(tc.tile_pool(name="hbp", bufs=4))
         rlp = ctx.enter_context(tc.tile_pool(name="rlp", bufs=10))
         resp = ctx.enter_context(tc.tile_pool(name="resp", bufs=4))
-        work = ctx.enter_context(tc.psum_pool(name="work", bufs=4))
+        bankp = ctx.enter_context(tc.psum_pool(name="bankp", bufs=1))
         sump = ctx.enter_context(tc.psum_pool(name="sump", bufs=1))
         ctx.enter_context(tc.manual_schedule())
+
+        free_banks = ["w%d" % b for b in range(6)]
+        a_bank = {}
+
+        def bank(shape, dtype, keep=False):
+            tag = free_banks[0]
+            free_banks.remove(tag)
+            if not keep:
+                free_banks.append(tag)
+            return tag, bankp.tile(shape, dtype, name=tag)
 
         ident32 = const.tile([P, P], F32, name="ident32")
         make_identity(nc, ident32[:])
@@ -61,29 +72,35 @@ def tile_nonlocalmp_pa_kernel(tc, F, W1, b1, W2, b2, out):
         w1s = const.tile([P, 2, 2, 2, 512], U8, name="w1s", align_bytes=64)
         w2c = const.tile([P, 2, C], U32, name="w2c", align_bytes=64)
         w2s = const.tile([P, 2, C], U8, name="w2s", align_bytes=64)
-        hc = const.tile([P, NODES, 2, ROWS], U32, name="hc", align_bytes=64)
-        hs = const.tile([P, NODES, 2, ROWS], U8, name="hs", align_bytes=64)
-        a4 = const.tile([P, 2, ROWS, 4], F32, name="a4")
-        b4 = const.tile([P, 2, ROWS, 4], F32, name="b4")
+        hc = const.tile([P, UNITS, 2, ROWS], U32, name="hc", align_bytes=64)
+        hs = const.tile([P, UNITS, 2, ROWS], U8, name="hs", align_bytes=64)
+        b4 = const.tile([P, 2, 2, NODES, HSETS, 4], F32, name="b4")
+        a4 = const.tile([P, 2, 2, HSETS, NODES, 4], F32, name="a4")
         b1c = const.tile([P, 2, 4], BF16, name="b1c")
         b2r = const.tile([P, 8], F32, name="b2r")
-        b2row = const.tile([P, C], BF16, name="b2row")
+        b2l = const.tile([P, 8], F32, name="b2l")
 
-        nc.sync.dma_start(out=bt[0:8, :], in_=b2.rearrange("(r c) -> r c", c=P))
-        nc.sync.dma_start(out=b1c[:], in_=b1.rearrange("(g p t) -> p g t", g=2, t=4))
-        nc.sync.dma_start(out=fsb[:], in_=f_flat.rearrange("(f p) c -> p f c", p=P))
         w1raw = {}
         w2raw = {}
+
+        def load_w1(g, ab, kp):
+            raw = rawp.tile([P, 4, 512], BF16, name="raw")
+            r0 = ab * C + kp * 512
+            nc.sync.dma_start(
+                out=raw[:],
+                in_=W1[r0 : r0 + 512, g * 512 : (g + 1) * 512].rearrange("(p j) w -> p j w", j=4),
+            )
+            w1raw[(g, ab, kp)] = raw
+
+        load_w1(0, 0, 0)
+        nc.sync.dma_start(out=fsb[:], in_=f_flat.rearrange("(f p) c -> p f c", p=P))
+        nc.sync.dma_start(out=bt[0:8, :], in_=b2.rearrange("(r c) -> r c", c=P))
+        nc.sync.dma_start(out=b1c[:], in_=b1.rearrange("(g p t) -> p g t", g=2, t=4))
         for g in range(2):
             for ab in range(2):
                 for kp in range(2):
-                    raw = rawp.tile([P, 4, 512], BF16, name="raw")
-                    r0 = ab * C + kp * 512
-                    nc.sync.dma_start(
-                        out=raw[:],
-                        in_=W1[r0 : r0 + 512, g * 512 : (g + 1) * 512].rearrange("(p j) w -> p j w", j=4),
-                    )
-                    w1raw[(g, ab, kp)] = raw
+                    if (g, ab, kp) != (0, 0, 0):
+                        load_w1(g, ab, kp)
         for ch in range(2):
             for g in range(2):
                 raw = rawp.tile([P, 4, 512], BF16, name="raw")
@@ -92,7 +109,6 @@ def tile_nonlocalmp_pa_kernel(tc, F, W1, b1, W2, b2, out):
                     in_=W2[g * 512 : (g + 1) * 512, ch * 512 : (ch + 1) * 512].rearrange("(p j) n -> p j n", j=4),
                 )
                 w2raw[(g, ch)] = raw
-        nc.sync.dma_start(out=b2row[:], in_=b2.partition_broadcast(P))
 
         def regroup(raw, vshare):
             gq = grpp.tile([P, 512, 4], BF16, name="gq", align_bytes=64)
@@ -119,81 +135,51 @@ def tile_nonlocalmp_pa_kernel(tc, F, W1, b1, W2, b2, out):
                 out=codes.bitcast(FP8X4), scales=scales, in_=gq[:].rearrange("p w t -> p (w t)")
             )
 
-        btp = work.tile([P, P], BF16, name="wk")
-        nc.tensor.transpose(btp[:], bt[:], identb[:])
-        nc.vector.tensor_scalar_mul(out=b2r[:], in0=btp[:, 0:8], scalar1=1.0 - SLOPE)
-
-        fsb32 = fsb[:].bitcast(F32)
-        fg32 = fg[:].bitcast(F32)
-        for kp in range(2):
-            xt = work.tile([P, 2, ROWS], F32, name="wk")
-            for f in range(2):
-                for u in range(2):
-                    nc.tensor.transpose(
-                        xt[:, u, f * P : (f + 1) * P],
-                        fsb32[:, f, kp * 256 + u : (kp + 1) * 256 : 2],
-                        ident32[:],
-                    )
-            nc.scalar.copy(out=fg32[:, kp], in_=xt[:].rearrange("p u c -> p c u"))
-        nc.vector.quantize_mx(
-            out=fc[:].rearrange("p k c -> p (k c)").bitcast(FP8X4),
-            scales=fs[:].rearrange("p k c -> p (k c)"),
-            in_=fg[:].rearrange("p k c t -> p (k c t)"),
-        )
-
-        def stage1_pe(g, ab, tiles):
-            if True:
-                for f in range(2):
-                    ps = work.tile([P, 4, P], F32, name="wk")
-                    for t in range(4):
-                        for kp in range(2):
-                            nc.tensor.matmul_mx(
-                                out=ps[:, t, :],
-                                lhsT=w1c[:, g, ab, kp, t * P : (t + 1) * P].bitcast(FP8X4),
-                                lhsT_scale=w1s[:, g, ab, kp, t * P : (t + 1) * P],
-                                rhs=fc[:, kp, f * P : (f + 1) * P].bitcast(FP8X4),
-                                rhs_scale=fs[:, kp, f * P : (f + 1) * P],
-                                start=(kp == 0),
-                                stop=(kp == 1),
-                            )
-                    tiles[(ab, f)] = ps
-
-        def evac_a(g, tiles):
-            for f in range(2):
-                nc.vector.tensor_tensor(
-                    out=a4[:, g, f * P : (f + 1) * P, :],
-                    in0=tiles[(0, f)][:].rearrange("p t r -> p r t"),
-                    in1=b1c[:, g, :].unsqueeze(1).to_broadcast([P, P, 4]),
-                    op=ALU.add,
-                )
-
-        def evac_b(g, tiles, second_on_vector):
-            nc.scalar.copy(out=b4[:, g, 0:P, :], in_=tiles[(1, 0)][:].rearrange("p t r -> p r t"))
-            if second_on_vector:
-                nc.vector.tensor_copy(out=b4[:, g, P:ROWS, :], in_=tiles[(1, 1)][:].rearrange("p t r -> p r t"))
-            else:
-                nc.scalar.copy(out=b4[:, g, P:ROWS, :], in_=tiles[(1, 1)][:].rearrange("p t r -> p r t"))
-
         def w1q(g, idx, gq):
             quant(gq, w1c[:, g, idx // 2, idx % 2, :], w1s[:, g, idx // 2, idx % 2, :])
 
-        st0 = {}
-        prev = None
-        for idx in range(4):
-            gq = regroup_w1(w1raw[(0, idx // 2, idx % 2)], VSHARE)
-            if prev is not None:
-                w1q(0, prev[1], prev[0])
-                if prev[1] == 1:
-                    stage1_pe(0, 0, st0)
-            prev = (gq, idx)
-        w1q(0, 3, prev[0])
-        stage1_pe(0, 1, st0)
+        def stage1_pe(ps, g, ab, f):
+            for t in range(4):
+                for kp in range(2):
+                    nc.tensor.matmul_mx(
+                        out=ps[:, t, :],
+                        lhsT=w1c[:, g, ab, kp, t * P : (t + 1) * P].bitcast(FP8X4),
+                        lhsT_scale=w1s[:, g, ab, kp, t * P : (t + 1) * P],
+                        rhs=fc[:, kp, f * P : (f + 1) * P].bitcast(FP8X4),
+                        rhs_scale=fs[:, kp, f * P : (f + 1) * P],
+                        start=(kp == 0),
+                        stop=(kp == 1),
+                    )
+
+        aps = {}
+        bps = {}
+
+        def stage1_a(f, g):
+            a_bank[(f, g)], ps = bank([P, 4, P], F32, True)
+            stage1_pe(ps, g, 0, f)
+            aps[(f, g)] = ps
+
+        def stage1_b(f, g):
+            ps = bank([P, 4, P], F32)[1]
+            stage1_pe(ps, g, 1, f)
+            bps[(f, g)] = ps
+
+        def evac_b(f, g):
+            nc.vector.tensor_tensor(
+                out=b4[:, f, g],
+                in0=bps[(f, g)][:].rearrange("p t (b j) -> p j b t", j=NODES),
+                in1=b1c[:, g, :].unsqueeze(1).unsqueeze(1).to_broadcast([P, NODES, HSETS, 4]),
+                op=ALU.add,
+            )
+
+        def copy_a(f, g):
+            nc.scalar.copy(out=a4[:, f, g], in_=aps[(f, g)][:].rearrange("p t (b i) -> p b i t", i=NODES))
 
         total = {}
-        for hb in range(2):
-            for ch in range(2):
-                total[(hb, ch)] = sump.tile([P, 512], F32, name="tot%d%d" % (hb, ch))
-        state = {"pending": None, "evac1": False, "w2": 0, "last_e": None, "ready": []}
+        state = {"last_e": None, "tag": 0}
+        pending = []
+        ready = []
+        to_combine = []
         tcount = {}
         utile = {}
         hbt = {}
@@ -203,7 +189,7 @@ def tile_nonlocalmp_pa_kernel(tc, F, W1, b1, W2, b2, out):
 
         def main_and_leaky(n):
             for k in range(4):
-                y = work.tile([P, 2, ROWS], F32, name="wk")
+                y = bank([P, 2, ROWS], F32)[1]
                 for mloc in range(2):
                     m = 2 * k + mloc
                     for g in range(2):
@@ -222,143 +208,233 @@ def tile_nonlocalmp_pa_kernel(tc, F, W1, b1, W2, b2, out):
                     nc.scalar.activation(
                         out=rl[:, 0, mloc, :], in_=y[:, mloc, :], func=ACT.Relu, bias=b2r[:, m : m + 1], scale=1.0 - SLOPE
                     )
-                if n not in V_COMBINE:
+                if n % 8 == 0:
+                    for mloc in range(2):
+                        m = 2 * k + mloc
+                        nc.scalar.activation(
+                            out=rl[:, 1, mloc, :], in_=y[:, mloc, :], func=ACT.Identity, bias=b2l[:, m : m + 1], scale=SLOPE
+                        )
+                elif n not in V_COMBINE:
                     nc.scalar.mul(out=rl[:, 1], in_=y[:], mul=SLOPE)
                 rlt[(n, k)] = rl
                 ytile[(n, k)] = y
 
-        def combine(n):
-            if n in V_COMBINE:
-                for k in range(4):
+        def combine(most):
+            for step in range(most):
+                if to_combine:
+                    n, k = to_combine[0]
+                    to_combine.remove((n, k))
                     rl = rlt[(n, k)]
                     nc.vector.scalar_tensor_tensor(
                         out=rl[:, 1], in0=ytile[(n, k)][:], scalar=SLOPE, in1=rl[:, 0], op0=ALU.mult, op1=ALU.add
                     )
 
+        def finish_half(f):
+            for ch in range(2):
+                res = resp.tile([P, 512], F32, name="res")
+                if f == 1 and ch == 1:
+                    nc.vector.tensor_copy(out=res[:], in_=total[(f, ch)][:])
+                else:
+                    nc.scalar.copy(out=res[:], in_=total[(f, ch)][:])
+                nc.sync.dma_start(
+                    out=out_flat[f * P : (f + 1) * P, ch * 512 : (ch + 1) * 512], in_=res[:]
+                )
+
         def sum_transposes(n):
-            for hb in range(2):
-                for m in range(8):
-                    ch, mm = m // 4, m % 4
+            f = n // 8
+            terms = 0
+            for v in range(8):
+                terms = terms + (1 if 8 * f + v in V_COMBINE else 2)
+            if n % 8 == 0:
+                for ch in range(2):
+                    total[(f, ch)] = sump.tile([P, 512], F32, name="tot%d" % ch)
+            for m in range(8):
+                ch, mm = m // 4, m % 4
+                for j2 in range(2):
                     for term in ([1] if n in V_COMBINE else [0, 1]):
-                        cnt = tcount.get((hb, ch), 0)
-                        tcount[(hb, ch)] = cnt + 1
+                        cnt = tcount.get((f, ch), 0)
+                        tcount[(f, ch)] = cnt + 1
                         nc.tensor.matmul(
-                            out=total[(hb, ch)][:, mm * P : (mm + 1) * P],
-                            lhsT=rlt[(n, m // 2)][:, term, m % 2, hb * P : (hb + 1) * P],
+                            out=total[(f, ch)][:, mm * P : (mm + 1) * P],
+                            lhsT=rlt[(n, m // 2)][:, term, m % 2, j2 * P : (j2 + 1) * P],
                             rhs=ident32[:],
                             is_transpose=True,
                             start=(cnt == 0),
-                            stop=(cnt == 4 * (2 * NODES - len(V_COMBINE)) - 1),
+                            stop=(cnt == 8 * terms - 1),
                         )
+            if n % 8 == 7:
+                finish_half(f)
 
         def stage2(n):
-            assert state["w2"] == 4
-            if state["last_e"] is not None:
-                combine(state["last_e"])
+            combine(4)
             main_and_leaky(n)
             if state["last_e"] is not None:
                 sum_transposes(state["last_e"])
             state["last_e"] = n
+            if n in V_COMBINE:
+                to_combine.extend([(n, k) for k in range(4)])
 
         def flush():
-            q = state["pending"]
-            if q is None:
-                return
-            state["pending"] = None
-            n, g = SEQ[q]
-            nc.vector.quantize_mx(
-                out=hc[:, n, g, :].bitcast(FP8X4), scales=hs[:, n, g, :], in_=hbt[q][:]
-            )
-            done_g[n] = done_g.get(n, 0) + 1
-            if done_g[n] == 2:
-                state["ready"] = state["ready"] + [(n, q)]
+            while pending:
+                q = pending[0]
+                pending.remove(q)
+                n, g = SEQ[q]
+                nc.vector.quantize_mx(
+                    out=hc[:, n, g, :].bitcast(FP8X4), scales=hs[:, n, g, :], in_=hbt[q][:]
+                )
+                done_g[n] = done_g.get(n, 0) + 1
+                if done_g[n] == 2:
+                    ready.append(n)
 
-        def emit_ready(q_now):
-            while state["ready"] and state["ready"][0][1] + LAG <= q_now:
-                stage2(state["ready"][0][0])
-                state["ready"] = state["ready"][1:]
+        def emit_ready(last=UNITS - 1):
+            while ready and ready[0] <= last:
+                n = ready[0]
+                ready.remove(n)
+                stage2(n)
 
         def h_add(q):
             n, g = SEQ[q]
-            assert g == 0 or state["evac1"]
-            u = up.tile([P, SETS, NODES, 4], F32, name="u")
+            f, jp = n // 8, n % 8
+            state["tag"] = 1 - state["tag"]
+            u = up.tile([P, 2, HSETS, NODES, 4], F32, name="u%d" % state["tag"])
             utile[q] = u
-            a_view = a4[:, g].rearrange("p (b i) t -> p b i t", i=NODES)
-            b_view = b4[:, g].rearrange("p (b j) t -> p b j t", j=NODES)
             nc.vector.tensor_tensor(
                 out=u[:],
-                in0=a_view,
-                in1=b_view[:, :, n, :].unsqueeze(2).to_broadcast([P, SETS, NODES, 4]),
+                in0=aps[(f, g)][:]
+                .rearrange("p t (b i) -> p b i t", i=NODES)
+                .unsqueeze(1)
+                .to_broadcast([P, 2, HSETS, NODES, 4]),
+                in1=b4[:, f, g, 2 * jp : 2 * jp + 2].unsqueeze(3).to_broadcast([P, 2, HSETS, NODES, 4]),
                 op=ALU.add,
             )
             flush()
 
-        def h_leaky(q):
-            uf = utile[q][:].rearrange("p b i t -> p (b i t)")
-            hb16 = hbp.tile([P, 4 * ROWS], BF16, name="hb16", align_bytes=64)
-            nc.vector.scalar_tensor_tensor(
-                out=hb16[:], in0=uf, scalar=SLOPE, in1=uf, op0=ALU.mult, op1=ALU.max
+        def g_add(q, j2):
+            n, g = SEQ[q]
+            f, jp = n // 8, n % 8
+            u = up.tile([P, HSETS, NODES, 4], F32, name="ug" if j2 == 0 else "u%d" % state["tag"])
+            utile[(q, j2)] = u
+            nc.gpsimd.tensor_tensor(
+                out=u[:],
+                in0=a4[:, f, g],
+                in1=b4[:, f, g, 2 * jp + j2].unsqueeze(2).to_broadcast([P, HSETS, NODES, 4]),
+                op=ALU.add,
             )
+
+        def h_leaky(q):
+            hb16 = hbp.tile([P, 4 * ROWS], BF16, name="hb16", align_bytes=64)
+            if q in G_TILES:
+                for j2 in (1, 0):
+                    uf = utile[(q, j2)][:].rearrange("p b i t -> p (b i t)")
+                    nc.vector.scalar_tensor_tensor(
+                        out=hb16[:, j2 * 512 : (j2 + 1) * 512], in0=uf, scalar=SLOPE, in1=uf, op0=ALU.mult, op1=ALU.max
+                    )
+            else:
+                uf = utile[q][:].rearrange("p j b i t -> p (j b i t)")
+                nc.vector.scalar_tensor_tensor(
+                    out=hb16[:], in0=uf, scalar=SLOPE, in1=uf, op0=ALU.mult, op1=ALU.max
+                )
             hbt[q] = hb16
-            state["pending"] = q
+            pending.append(q)
 
         W2ORDER = [(0, 0), (1, 0), (0, 1), (1, 1)]
 
         def qw2(idx, gq):
             gg, ch = W2ORDER[idx]
             quant(gq, w2c[:, gg, ch * 512 : (ch + 1) * 512], w2s[:, gg, ch * 512 : (ch + 1) * 512])
-            state["w2"] = state["w2"] + 1
 
-        st1 = {}
+        g00 = regroup_w1(w1raw[(0, 0, 0)], VSHARE)
+
+        fsb32 = fsb[:].bitcast(F32)
+        fg32 = fg[:].bitcast(F32)
+        for kp in range(2):
+            xt = bank([P, 2, ROWS], F32)[1]
+            for f in range(2):
+                for u in range(2):
+                    nc.tensor.transpose(
+                        xt[:, u, f * P : (f + 1) * P],
+                        fsb32[:, f, kp * 256 + u : (kp + 1) * 256 : 2],
+                        ident32[:],
+                    )
+            nc.scalar.copy(out=fg32[:, kp], in_=xt[:].rearrange("p u c -> p c u"))
+        btp = bank([P, P], BF16)[1]
+        nc.tensor.transpose(btp[:], bt[:], identb[:])
+
+        g01 = regroup_w1(w1raw[(0, 0, 1)], VSHARE)
+        w1q(0, 0, g00)
+        g02 = regroup_w1(w1raw[(0, 1, 0)], VSHARE)
+        nc.vector.quantize_mx(
+            out=fc[:].rearrange("p k c -> p (k c)").bitcast(FP8X4),
+            scales=fs[:].rearrange("p k c -> p (k c)"),
+            in_=fg[:].rearrange("p k c t -> p (k c t)"),
+        )
+        w1q(0, 1, g01)
+        stage1_a(0, 0)
+        g03 = regroup_w1(w1raw[(0, 1, 1)], VSHARE)
+        w1q(0, 2, g02)
+        nc.vector.tensor_scalar_mul(out=b2r[:], in0=btp[:, 0:8], scalar1=1.0 - SLOPE)
+        nc.vector.tensor_scalar_mul(out=b2l[:], in0=btp[:, 0:8], scalar1=SLOPE * NODES / 2)
+        w1q(0, 3, g03)
+        stage1_b(0, 0)
+
         g10 = regroup_w1(w1raw[(1, 0, 0)], 0)
-        evac_a(0, st0)
-        evac_b(0, st0, False)
         g11 = regroup_w1(w1raw[(1, 0, 1)], 128)
+        evac_b(0, 0)
         g12 = regroup_w1(w1raw[(1, 1, 0)], 0)
-        w1q(1, 0, g10)
         w1q(1, 1, g11)
-        stage1_pe(1, 0, st1)
         h_add(0)
+        w1q(1, 0, g10)
+        stage1_a(0, 1)
         g13 = regroup_w1(w1raw[(1, 1, 1)], 128)
         w2a = regroup(w2raw[W2ORDER[0]], 0)
-        w2b = regroup(w2raw[W2ORDER[1]], 0)
-        w1q(1, 2, g12)
-        w1q(1, 3, g13)
-        stage1_pe(1, 1, st1)
         h_leaky(0)
-        evac_b(1, st1, False)
-        evac_a(1, st1)
-        state["evac1"] = True
+        w1q(1, 3, g13)
+        w1q(1, 2, g12)
+        stage1_b(0, 1)
+        w2b = regroup(w2raw[W2ORDER[1]], 0)
         flush()
+        evac_b(0, 1)
         w2c_ = regroup(w2raw[W2ORDER[2]], 0)
         w2d_ = regroup(w2raw[W2ORDER[3]], 0)
-        h_add(1)
+        stage1_b(1, 0)
+        stage1_b(1, 1)
         qw2(0, w2a)
+        h_add(1)
         qw2(1, w2b)
         h_leaky(1)
+        h_add(2)
         qw2(2, w2c_)
-        flush()
+        h_leaky(2)
         qw2(3, w2d_)
-        for q in range(2, len(SEQ)):
-            h_add(q)
-            emit_ready(q)
-            h_leaky(q)
+        copy_a(0, 0)
+        copy_a(0, 1)
+        emit_ready(HELD)
+        h_add(3)
+        h_leaky(3)
+        g_add(G_TILES[0], 0)
+        emit_ready(HELD)
+        for q in range(4, len(SEQ)):
+            if q == 4:
+                evac_b(1, 0)
+                evac_b(1, 1)
+            if q in (QA, QA + 1):
+                stage1_a(1, q - QA)
+                copy_a(1, q - QA)
+            if q in G_TILES:
+                h_leaky(q)
+                if q + 3 in G_TILES:
+                    g_add(q + 3, 0)
+            else:
+                h_add(q)
+                if q == 14:
+                    free_banks.append(a_bank[(0, 0)])
+                    free_banks.append(a_bank[(0, 1)])
+                emit_ready(HELD)
+                h_leaky(q)
+                combine(2)
+                if q + 2 in G_TILES:
+                    g_add(q + 2, 1)
         flush()
-        emit_ready(len(SEQ) + LAG)
-        combine(state["last_e"])
+        emit_ready()
+        combine(4)
         sum_transposes(state["last_e"])
-
-        for ch in range(2):
-            for hb in range(2):
-                res = resp.tile([P, 512], F32, name="res")
-                nc.vector.scalar_tensor_tensor(
-                    out=res[:],
-                    in0=b2row[:, ch * 512 : (ch + 1) * 512],
-                    scalar=SLOPE * NODES,
-                    in1=total[(hb, ch)][:],
-                    op0=ALU.mult,
-                    op1=ALU.add,
-                )
-                nc.sync.dma_start(
-                    out=out_flat[hb * P : (hb + 1) * P, ch * 512 : (ch + 1) * 512], in_=res[:]
-                )

@@ -24,10 +24,9 @@ FLOPS = 2 * ROWS * C * 2 * C + 2 * ROWS * NODES * C * C
 
 SEQ = [(n, g) for n in range(UNITS) for g in range(2)]
 VSHARE = 84
-V_COMBINE = [11, 12, 13, 14, 15]
+V_COMBINE = [13, 14, 15]
 QA = 12
 HELD = min(V_COMBINE) - 1
-G_TILES = [6, 9, 12, 15, 18, 21, 24, 27, 30]
 
 
 def tile_nonlocalmp_pa_kernel(tc, F, W1, b1, W2, b2, out):
@@ -75,7 +74,6 @@ def tile_nonlocalmp_pa_kernel(tc, F, W1, b1, W2, b2, out):
         hc = const.tile([P, UNITS, 2, ROWS], U32, name="hc", align_bytes=64)
         hs = const.tile([P, UNITS, 2, ROWS], U8, name="hs", align_bytes=64)
         b4 = const.tile([P, 2, 2, NODES, HSETS, 4], F32, name="b4")
-        a4 = const.tile([P, 2, 2, HSETS, NODES, 4], F32, name="a4")
         b1c = const.tile([P, 2, 4], BF16, name="b1c")
         b2r = const.tile([P, 8], F32, name="b2r")
         b2l = const.tile([P, 8], F32, name="b2l")
@@ -171,9 +169,6 @@ def tile_nonlocalmp_pa_kernel(tc, F, W1, b1, W2, b2, out):
                 in1=b1c[:, g, :].unsqueeze(1).unsqueeze(1).to_broadcast([P, NODES, HSETS, 4]),
                 op=ALU.add,
             )
-
-        def copy_a(f, g):
-            nc.scalar.copy(out=a4[:, f, g], in_=aps[(f, g)][:].rearrange("p t (b i) -> p b i t", i=NODES))
 
         total = {}
         state = {"last_e": None, "tag": 0}
@@ -309,31 +304,12 @@ def tile_nonlocalmp_pa_kernel(tc, F, W1, b1, W2, b2, out):
             )
             flush()
 
-        def g_add(q, j2):
-            n, g = SEQ[q]
-            f, jp = n // 8, n % 8
-            u = up.tile([P, HSETS, NODES, 4], F32, name="ug" if j2 == 0 else "u%d" % state["tag"])
-            utile[(q, j2)] = u
-            nc.gpsimd.tensor_tensor(
-                out=u[:],
-                in0=a4[:, f, g],
-                in1=b4[:, f, g, 2 * jp + j2].unsqueeze(2).to_broadcast([P, HSETS, NODES, 4]),
-                op=ALU.add,
-            )
-
         def h_leaky(q):
             hb16 = hbp.tile([P, 4 * ROWS], BF16, name="hb16", align_bytes=64)
-            if q in G_TILES:
-                for j2 in (1, 0):
-                    uf = utile[(q, j2)][:].rearrange("p b i t -> p (b i t)")
-                    nc.vector.scalar_tensor_tensor(
-                        out=hb16[:, j2 * 512 : (j2 + 1) * 512], in0=uf, scalar=SLOPE, in1=uf, op0=ALU.mult, op1=ALU.max
-                    )
-            else:
-                uf = utile[q][:].rearrange("p j b i t -> p (j b i t)")
-                nc.vector.scalar_tensor_tensor(
-                    out=hb16[:], in0=uf, scalar=SLOPE, in1=uf, op0=ALU.mult, op1=ALU.max
-                )
+            uf = utile[q][:].rearrange("p j b i t -> p (j b i t)")
+            nc.vector.scalar_tensor_tensor(
+                out=hb16[:], in0=uf, scalar=SLOPE, in1=uf, op0=ALU.mult, op1=ALU.max
+            )
             hbt[q] = hb16
             pending.append(q)
 
@@ -406,34 +382,21 @@ def tile_nonlocalmp_pa_kernel(tc, F, W1, b1, W2, b2, out):
         qw2(2, w2c_)
         h_leaky(2)
         qw2(3, w2d_)
-        copy_a(0, 0)
-        copy_a(0, 1)
         emit_ready(HELD)
         h_add(3)
         h_leaky(3)
-        g_add(G_TILES[0], 0)
         emit_ready(HELD)
         for q in range(4, len(SEQ)):
-            if q == 4:
-                evac_b(1, 0)
-                evac_b(1, 1)
+            if q in (4, 5):
+                evac_b(1, q - 4)
             if q in (QA, QA + 1):
                 stage1_a(1, q - QA)
-                copy_a(1, q - QA)
-            if q in G_TILES:
-                h_leaky(q)
-                if q + 3 in G_TILES:
-                    g_add(q + 3, 0)
-            else:
-                h_add(q)
-                if q == 14:
-                    free_banks.append(a_bank[(0, 0)])
-                    free_banks.append(a_bank[(0, 1)])
-                emit_ready(HELD)
-                h_leaky(q)
-                combine(2)
-                if q + 2 in G_TILES:
-                    g_add(q + 2, 1)
+            h_add(q)
+            if q in (14, 15):
+                free_banks.append(a_bank[(0, q - 14)])
+            emit_ready(HELD)
+            h_leaky(q)
+            combine(2)
         flush()
         emit_ready()
         combine(4)

@@ -24,9 +24,11 @@ FLOPS = 2 * ROWS * C * 2 * C + 2 * ROWS * NODES * C * C
 
 SEQ = [(n, g) for n in range(UNITS) for g in range(2)]
 VSHARE = 84
-V_COMBINE = [13, 14, 15]
+V_LEAKY = [13, 14, 15]
 QA = 12
-HELD = min(V_COMBINE) - 1
+DELAY = 6
+GROUP = 4
+QB = 10
 
 
 def tile_nonlocalmp_pa_kernel(tc, F, W1, b1, W2, b2, out):
@@ -40,7 +42,7 @@ def tile_nonlocalmp_pa_kernel(tc, F, W1, b1, W2, b2, out):
         grpp = ctx.enter_context(tc.tile_pool(name="grpp", bufs=4))
         up = ctx.enter_context(tc.tile_pool(name="up", bufs=1))
         hbp = ctx.enter_context(tc.tile_pool(name="hbp", bufs=4))
-        rlp = ctx.enter_context(tc.tile_pool(name="rlp", bufs=10))
+        rlp = ctx.enter_context(tc.tile_pool(name="rlp", bufs=16))
         resp = ctx.enter_context(tc.tile_pool(name="resp", bufs=4))
         bankp = ctx.enter_context(tc.psum_pool(name="bankp", bufs=1))
         sump = ctx.enter_context(tc.psum_pool(name="sump", bufs=1))
@@ -76,7 +78,8 @@ def tile_nonlocalmp_pa_kernel(tc, F, W1, b1, W2, b2, out):
         b4 = const.tile([P, 2, 2, NODES, HSETS, 4], F32, name="b4")
         b1c = const.tile([P, 2, 4], BF16, name="b1c")
         b2r = const.tile([P, 8], F32, name="b2r")
-        b2l = const.tile([P, 8], F32, name="b2l")
+        b2v = const.tile([P, 8], F32, name="b2v")
+        b2l = [const.tile([P, 8], F32, name="b2l%d" % f) for f in range(2)]
 
         w1raw = {}
         w2raw = {}
@@ -91,13 +94,14 @@ def tile_nonlocalmp_pa_kernel(tc, F, W1, b1, W2, b2, out):
             w1raw[(g, ab, kp)] = raw
 
         load_w1(0, 0, 0)
+        load_w1(0, 0, 1)
         nc.sync.dma_start(out=fsb[:], in_=f_flat.rearrange("(f p) c -> p f c", p=P))
         nc.sync.dma_start(out=bt[0:8, :], in_=b2.rearrange("(r c) -> r c", c=P))
         nc.sync.dma_start(out=b1c[:], in_=b1.rearrange("(g p t) -> p g t", g=2, t=4))
         for g in range(2):
             for ab in range(2):
                 for kp in range(2):
-                    if (g, ab, kp) != (0, 0, 0):
+                    if (g, ab, kp) not in ((0, 0, 0), (0, 0, 1)):
                         load_w1(g, ab, kp)
         for ch in range(2):
             for g in range(2):
@@ -170,104 +174,125 @@ def tile_nonlocalmp_pa_kernel(tc, F, W1, b1, W2, b2, out):
                 op=ALU.add,
             )
 
+        def add_b1(g):
+            nc.vector.tensor_tensor(
+                out=b4[:, 1, g],
+                in0=b4[:, 1, g],
+                in1=b1c[:, g, :].unsqueeze(1).unsqueeze(1).to_broadcast([P, NODES, HSETS, 4]),
+                op=ALU.add,
+            )
+
         total = {}
-        state = {"last_e": None, "tag": 0}
+        state = {"tag": 0}
+        banks = [(n, k) for n in range(UNITS) for k in range(4)]
+        groups = []
+        while banks:
+            groups.append(banks[0:GROUP])
+            banks = banks[GROUP:]
+        to_sum = []
+        to_leaky = []
         pending = []
         ready = []
-        to_combine = []
         tcount = {}
         utile = {}
         hbt = {}
         rlt = {}
-        ytile = {}
         done_g = {}
 
-        def main_and_leaky(n):
-            for k in range(4):
-                y = bank([P, 2, ROWS], F32)[1]
-                for mloc in range(2):
-                    m = 2 * k + mloc
-                    for g in range(2):
-                        nc.tensor.matmul_mx(
-                            out=y[:, mloc, :],
-                            lhsT=w2c[:, g, m * P : (m + 1) * P].bitcast(FP8X4),
-                            lhsT_scale=w2s[:, g, m * P : (m + 1) * P],
-                            rhs=hc[:, n, g, :].bitcast(FP8X4),
-                            rhs_scale=hs[:, n, g, :],
-                            start=(g == 0),
-                            stop=(g == 1),
-                        )
-                rl = rlp.tile([P, 2, 2, ROWS], F32, name="rl")
-                for mloc in range(2):
-                    m = 2 * k + mloc
+        def main_and_leaky(n, k):
+            y = bank([P, 2, ROWS], F32)[1]
+            for mloc in range(2):
+                m = 2 * k + mloc
+                for g in range(2):
+                    nc.tensor.matmul_mx(
+                        out=y[:, mloc, :],
+                        lhsT=w2c[:, g, m * P : (m + 1) * P].bitcast(FP8X4),
+                        lhsT_scale=w2s[:, g, m * P : (m + 1) * P],
+                        rhs=hc[:, n, g, :].bitcast(FP8X4),
+                        rhs_scale=hs[:, n, g, :],
+                        start=(g == 0),
+                        stop=(g == 1),
+                    )
+            rl = rlp.tile([P, 2, 2, ROWS], F32, name="rl")
+            rlt[(n, k)] = rl
+            for mloc in range(2):
+                m = 2 * k + mloc
+                if n in V_LEAKY:
+                    nc.scalar.activation(
+                        out=rl[:, 0, mloc, :], in_=y[:, mloc, :], func=ACT.Identity, bias=b2v[:, m : m + 1], scale=1.0
+                    )
+                else:
                     nc.scalar.activation(
                         out=rl[:, 0, mloc, :], in_=y[:, mloc, :], func=ACT.Relu, bias=b2r[:, m : m + 1], scale=1.0 - SLOPE
                     )
-                if n % 8 == 0:
-                    for mloc in range(2):
-                        m = 2 * k + mloc
-                        nc.scalar.activation(
-                            out=rl[:, 1, mloc, :], in_=y[:, mloc, :], func=ACT.Identity, bias=b2l[:, m : m + 1], scale=SLOPE
-                        )
-                elif n not in V_COMBINE:
-                    nc.scalar.mul(out=rl[:, 1], in_=y[:], mul=SLOPE)
-                rlt[(n, k)] = rl
-                ytile[(n, k)] = y
-
-        def combine(most):
-            for step in range(most):
-                if to_combine:
-                    n, k = to_combine[0]
-                    to_combine.remove((n, k))
-                    rl = rlt[(n, k)]
-                    nc.vector.scalar_tensor_tensor(
-                        out=rl[:, 1], in0=ytile[(n, k)][:], scalar=SLOPE, in1=rl[:, 0], op0=ALU.mult, op1=ALU.add
+            if n in V_LEAKY:
+                return
+            if n % 8 == 0:
+                for mloc in range(2):
+                    m = 2 * k + mloc
+                    nc.scalar.activation(
+                        out=rl[:, 1, mloc, :], in_=y[:, mloc, :], func=ACT.Identity, bias=b2l[n // 8][:, m : m + 1], scale=SLOPE
                     )
+            else:
+                nc.scalar.mul(out=rl[:, 1], in_=y[:], mul=SLOPE)
 
-        def finish_half(f):
-            for ch in range(2):
-                res = resp.tile([P, 512], F32, name="res")
-                if f == 1 and ch == 1:
-                    nc.vector.tensor_copy(out=res[:], in_=total[(f, ch)][:])
-                else:
-                    nc.scalar.copy(out=res[:], in_=total[(f, ch)][:])
-                nc.sync.dma_start(
-                    out=out_flat[f * P : (f + 1) * P, ch * 512 : (ch + 1) * 512], in_=res[:]
-                )
+        def v_leaky(n, k):
+            rl = rlt[(n, k)]
+            nc.vector.scalar_tensor_tensor(
+                out=rl[:, 1], in0=rl[:, 0], scalar=SLOPE, in1=rl[:, 0], op0=ALU.mult, op1=ALU.max
+            )
 
-        def sum_transposes(n):
-            f = n // 8
+        def finish(f, ch):
+            res = resp.tile([P, 512], F32, name="res")
+            if f == 1:
+                nc.vector.tensor_copy(out=res[:], in_=total[(f, ch)][:])
+            else:
+                nc.scalar.copy(out=res[:], in_=total[(f, ch)][:])
+            nc.sync.dma_start(
+                out=out_flat[f * P : (f + 1) * P, ch * 512 : (ch + 1) * 512], in_=res[:]
+            )
+
+        def sum_transposes(n, k):
+            f, ch = n // 8, k // 2
             terms = 0
             for v in range(8):
-                terms = terms + (1 if 8 * f + v in V_COMBINE else 2)
-            if n % 8 == 0:
-                for ch in range(2):
-                    total[(f, ch)] = sump.tile([P, 512], F32, name="tot%d" % ch)
-            for m in range(8):
-                ch, mm = m // 4, m % 4
+                terms = terms + (1 if 8 * f + v in V_LEAKY else 2)
+            if (f, ch) not in total:
+                total[(f, ch)] = sump.tile([P, 512], F32, name="tot%d" % ch)
+            for m in (2 * k, 2 * k + 1):
+                mm = m % 4
                 for j2 in range(2):
-                    for term in ([1] if n in V_COMBINE else [0, 1]):
+                    for term in ([1] if n in V_LEAKY else [0, 1]):
                         cnt = tcount.get((f, ch), 0)
                         tcount[(f, ch)] = cnt + 1
                         nc.tensor.matmul(
                             out=total[(f, ch)][:, mm * P : (mm + 1) * P],
-                            lhsT=rlt[(n, m // 2)][:, term, m % 2, j2 * P : (j2 + 1) * P],
+                            lhsT=rlt[(n, k)][:, term, m % 2, j2 * P : (j2 + 1) * P],
                             rhs=ident32[:],
                             is_transpose=True,
                             start=(cnt == 0),
                             stop=(cnt == 8 * terms - 1),
                         )
-            if n % 8 == 7:
-                finish_half(f)
+            if tcount[(f, ch)] == 8 * terms:
+                finish(f, ch)
 
-        def stage2(n):
-            combine(4)
-            main_and_leaky(n)
-            if state["last_e"] is not None:
-                sum_transposes(state["last_e"])
-            state["last_e"] = n
-            if n in V_COMBINE:
-                to_combine.extend([(n, k) for k in range(4)])
+        def leaky_due(q):
+            while to_leaky and 2 * to_leaky[0][0] + DELAY + to_leaky[0][1] // 2 <= q:
+                n, k = to_leaky[0]
+                to_leaky.remove((n, k))
+                v_leaky(n, k)
+
+        def run_group(group, q):
+            for n, k in group:
+                main_and_leaky(n, k)
+                if n in V_LEAKY:
+                    to_leaky.append((n, k))
+            leaky_due(q)
+            for n, k in list(to_sum):
+                if (n, k) not in to_leaky:
+                    to_sum.remove((n, k))
+                    sum_transposes(n, k)
+            to_sum.extend(group)
 
         def flush():
             while pending:
@@ -281,11 +306,11 @@ def tile_nonlocalmp_pa_kernel(tc, F, W1, b1, W2, b2, out):
                 if done_g[n] == 2:
                     ready.append(n)
 
-        def emit_ready(last=UNITS - 1):
-            while ready and ready[0] <= last:
-                n = ready[0]
-                ready.remove(n)
-                stage2(n)
+        def emit_ready(q):
+            while groups and groups[0][-1][0] in ready:
+                group = groups[0]
+                groups.remove(group)
+                run_group(group, q)
 
         def h_add(q):
             n, g = SEQ[q]
@@ -349,7 +374,10 @@ def tile_nonlocalmp_pa_kernel(tc, F, W1, b1, W2, b2, out):
         g03 = regroup_w1(w1raw[(0, 1, 1)], VSHARE)
         w1q(0, 2, g02)
         nc.vector.tensor_scalar_mul(out=b2r[:], in0=btp[:, 0:8], scalar1=1.0 - SLOPE)
-        nc.vector.tensor_scalar_mul(out=b2l[:], in0=btp[:, 0:8], scalar1=SLOPE * NODES / 2)
+        nc.vector.tensor_copy(out=b2v[:], in_=btp[:, 0:8])
+        for f in range(2):
+            plain = len([n for n in range(8 * f, 8 * f + 8) if n not in V_LEAKY])
+            nc.vector.tensor_scalar_mul(out=b2l[f][:], in0=btp[:, 0:8], scalar1=SLOPE * plain)
         w1q(0, 3, g03)
         stage1_b(0, 0)
 
@@ -369,35 +397,38 @@ def tile_nonlocalmp_pa_kernel(tc, F, W1, b1, W2, b2, out):
         stage1_b(0, 1)
         w2b = regroup(w2raw[W2ORDER[1]], 0)
         flush()
+        qw2(0, w2a)
         evac_b(0, 1)
+        for g in range(2):
+            stage1_b(1, g)
+            nc.scalar.copy(out=b4[:, 1, g], in_=bps[(1, g)][:].rearrange("p t (b j) -> p j b t", j=NODES))
         w2c_ = regroup(w2raw[W2ORDER[2]], 0)
         w2d_ = regroup(w2raw[W2ORDER[3]], 0)
-        stage1_b(1, 0)
-        stage1_b(1, 1)
-        qw2(0, w2a)
         h_add(1)
-        qw2(1, w2b)
-        h_leaky(1)
         h_add(2)
-        qw2(2, w2c_)
+        h_leaky(1)
+        qw2(1, w2b)
+        flush()
         h_leaky(2)
-        qw2(3, w2d_)
-        emit_ready(HELD)
         h_add(3)
+        qw2(2, w2c_)
+        qw2(3, w2d_)
+        emit_ready(3)
         h_leaky(3)
-        emit_ready(HELD)
+        emit_ready(3)
         for q in range(4, len(SEQ)):
-            if q in (4, 5):
-                evac_b(1, q - 4)
+            if q in (QB, QB + 1):
+                add_b1(q - QB)
             if q in (QA, QA + 1):
                 stage1_a(1, q - QA)
             h_add(q)
             if q in (14, 15):
                 free_banks.append(a_bank[(0, q - 14)])
-            emit_ready(HELD)
+            emit_ready(q)
             h_leaky(q)
-            combine(2)
+            leaky_due(q)
         flush()
-        emit_ready()
-        combine(4)
-        sum_transposes(state["last_e"])
+        emit_ready(3 * len(SEQ))
+        leaky_due(3 * len(SEQ))
+        for n, k in to_sum:
+            sum_transposes(n, k)

@@ -124,12 +124,12 @@ def tile_nonlocalmp_pa_kernel(tc, F, W1, b1, W2, b2, out):
 
         def regroup_w1(raw, vshare):
             gq = grpp.tile([P, 512, 4], BF16, name="gq", align_bytes=64)
-            dst = gq[:].rearrange("p (t m) j -> p t m j", t=4)
-            src = raw[:].rearrange("p j (m t) -> p t m j", t=4)
+            dst = gq[:].rearrange("p (t m) j -> p m j t", t=4)
+            src = raw[:].rearrange("p j (m t) -> p m j t", t=4)
             if vshare > 0:
-                nc.vector.tensor_copy(out=dst[:, :, 0:vshare], in_=src[:, :, 0:vshare])
+                nc.vector.tensor_copy(out=dst[:, 0:vshare], in_=src[:, 0:vshare])
             if vshare < 128:
-                nc.scalar.copy(out=dst[:, :, vshare:128], in_=src[:, :, vshare:128])
+                nc.scalar.copy(out=dst[:, vshare:128], in_=src[:, vshare:128])
             return gq
 
         def quant(gq, codes, scales):

@@ -24,9 +24,14 @@ FLOPS = 2 * ROWS * C * 2 * C + 2 * ROWS * NODES * C * C
 
 SEQ = [(n, g) for n in range(UNITS) for g in range(2)]
 VSHARE = 84
-V_LEAKY = [13, 14, 15]
+V_LEAKY = [12, 13, 14, 15]
+G_TILES = [9, 14, 19, 24, 29]
+G_PIECES = [[(0, 0, 4)], [(0, 4, 8)], [(1, 0, 4)], [(1, 4, 8)]]
+G_LEAD = 5
+U_SLOTS = 7
+H_SLOTS = 8
 QA = 12
-DELAY = 6
+DELAY = 7
 GROUP = 4
 QB = 10
 
@@ -41,6 +46,7 @@ def tile_nonlocalmp_pa_kernel(tc, F, W1, b1, W2, b2, out):
         rawp = ctx.enter_context(tc.tile_pool(name="rawp", bufs=8))
         grpp = ctx.enter_context(tc.tile_pool(name="grpp", bufs=4))
         up = ctx.enter_context(tc.tile_pool(name="up", bufs=1))
+        hqp = ctx.enter_context(tc.tile_pool(name="hqp", bufs=H_SLOTS))
         hbp = ctx.enter_context(tc.tile_pool(name="hbp", bufs=4))
         rlp = ctx.enter_context(tc.tile_pool(name="rlp", bufs=16))
         resp = ctx.enter_context(tc.tile_pool(name="resp", bufs=4))
@@ -73,8 +79,8 @@ def tile_nonlocalmp_pa_kernel(tc, F, W1, b1, W2, b2, out):
         w1s = const.tile([P, 2, 2, 2, 512], U8, name="w1s", align_bytes=64)
         w2c = const.tile([P, 2, C], U32, name="w2c", align_bytes=64)
         w2s = const.tile([P, 2, C], U8, name="w2s", align_bytes=64)
-        hc = const.tile([P, UNITS, 2, ROWS], U32, name="hc", align_bytes=64)
-        hs = const.tile([P, UNITS, 2, ROWS], U8, name="hs", align_bytes=64)
+        hcode = {}
+        a4 = const.tile([P, 2, 2, HSETS, NODES, 4], F32, name="a4")
         b4 = const.tile([P, 2, 2, NODES, HSETS, 4], F32, name="b4")
         b1c = const.tile([P, 2, 4], BF16, name="b1c")
         b2r = const.tile([P, 8], F32, name="b2r")
@@ -166,6 +172,9 @@ def tile_nonlocalmp_pa_kernel(tc, F, W1, b1, W2, b2, out):
             stage1_pe(ps, g, 1, f)
             bps[(f, g)] = ps
 
+        def copy_a(f, g):
+            nc.scalar.copy(out=a4[:, f, g], in_=aps[(f, g)][:].rearrange("p t (b i) -> p b i t", i=NODES))
+
         def evac_b(f, g):
             nc.vector.tensor_tensor(
                 out=b4[:, f, g],
@@ -183,7 +192,10 @@ def tile_nonlocalmp_pa_kernel(tc, F, W1, b1, W2, b2, out):
             )
 
         total = {}
-        state = {"tag": 0}
+        u_free = ["u%d" % b for b in range(U_SLOTS)]
+        u_tag = {}
+        gpieces = {}
+        g_todo = [(q, piece) for q in G_TILES for piece in G_PIECES]
         banks = [(n, k) for n in range(UNITS) for k in range(4)]
         groups = []
         while banks:
@@ -208,8 +220,8 @@ def tile_nonlocalmp_pa_kernel(tc, F, W1, b1, W2, b2, out):
                         out=y[:, mloc, :],
                         lhsT=w2c[:, g, m * P : (m + 1) * P].bitcast(FP8X4),
                         lhsT_scale=w2s[:, g, m * P : (m + 1) * P],
-                        rhs=hc[:, n, g, :].bitcast(FP8X4),
-                        rhs_scale=hs[:, n, g, :],
+                        rhs=hcode[n][0][:, g, :].bitcast(FP8X4),
+                        rhs_scale=hcode[n][1][:, g, :],
                         start=(g == 0),
                         stop=(g == 1),
                     )
@@ -299,8 +311,13 @@ def tile_nonlocalmp_pa_kernel(tc, F, W1, b1, W2, b2, out):
                 q = pending[0]
                 pending.remove(q)
                 n, g = SEQ[q]
+                if n not in hcode:
+                    hcode[n] = (
+                        hqp.tile([P, 2, ROWS], U32, name="hc", align_bytes=64),
+                        hqp.tile([P, 2, ROWS], U8, name="hs", align_bytes=64),
+                    )
                 nc.vector.quantize_mx(
-                    out=hc[:, n, g, :].bitcast(FP8X4), scales=hs[:, n, g, :], in_=hbt[q][:]
+                    out=hcode[n][0][:, g, :].bitcast(FP8X4), scales=hcode[n][1][:, g, :], in_=hbt[q][:]
                 )
                 done_g[n] = done_g.get(n, 0) + 1
                 if done_g[n] == 2:
@@ -315,8 +332,10 @@ def tile_nonlocalmp_pa_kernel(tc, F, W1, b1, W2, b2, out):
         def h_add(q):
             n, g = SEQ[q]
             f, jp = n // 8, n % 8
-            state["tag"] = 1 - state["tag"]
-            u = up.tile([P, 2, HSETS, NODES, 4], F32, name="u%d" % state["tag"])
+            tag = u_free[0]
+            u_free.remove(tag)
+            u_tag[q] = tag
+            u = up.tile([P, 2, HSETS, NODES, 4], F32, name=tag)
             utile[q] = u
             nc.vector.tensor_tensor(
                 out=u[:],
@@ -329,14 +348,47 @@ def tile_nonlocalmp_pa_kernel(tc, F, W1, b1, W2, b2, out):
             )
             flush()
 
+        def leaky_piece(dst, src):
+            nc.vector.scalar_tensor_tensor(out=dst, in0=src, scalar=SLOPE, in1=src, op0=ALU.mult, op1=ALU.max)
+
+        def g_piece(tag):
+            q, piece = g_todo[0]
+            g_todo.remove((q, piece))
+            n, g = SEQ[q]
+            f, jp = n // 8, n % 8
+            ug = up.tile([P, sum([b1 - b0 for jj, b0, b1 in piece]), NODES, 4], F32, name=tag)
+            gpieces.setdefault(q, []).append((ug, tag, sum([b1 - b0 for jj, b0, b1 in piece]) * NODES * 4))
+            at = 0
+            for jj, b0, b1 in piece:
+                nc.gpsimd.tensor_tensor(
+                    out=ug[:, at : at + b1 - b0],
+                    in0=a4[:, f, g, b0:b1],
+                    in1=b4[:, f, g, 2 * jp + jj, b0:b1].unsqueeze(2).to_broadcast([P, b1 - b0, NODES, 4]),
+                    op=ALU.add,
+                )
+                at = at + b1 - b0
+
+        def release(tag, q):
+            if g_todo and g_todo[0][0] - G_LEAD <= q:
+                g_piece(tag)
+            else:
+                u_free.append(tag)
+
         def h_leaky(q):
             hb16 = hbp.tile([P, 4 * ROWS], BF16, name="hb16", align_bytes=64)
-            uf = utile[q][:].rearrange("p j b i t -> p (j b i t)")
-            nc.vector.scalar_tensor_tensor(
-                out=hb16[:], in0=uf, scalar=SLOPE, in1=uf, op0=ALU.mult, op1=ALU.max
-            )
             hbt[q] = hb16
             pending.append(q)
+            if q in G_TILES:
+                at = 0
+                for ug, tag, size in gpieces[q]:
+                    leaky_piece(hb16[:, at : at + size], ug[:].rearrange("p b i t -> p (b i t)"))
+                    at = at + size
+                for ug, tag, size in gpieces[q][0:-1]:
+                    u_free.append(tag)
+                release(gpieces[q][-1][1], q)
+                return
+            leaky_piece(hb16[:], utile[q][:].rearrange("p j b i t -> p (j b i t)"))
+            release(u_tag[q], q)
 
         W2ORDER = [(0, 0), (1, 0), (0, 1), (1, 1)]
 
@@ -406,11 +458,13 @@ def tile_nonlocalmp_pa_kernel(tc, F, W1, b1, W2, b2, out):
         w2d_ = regroup(w2raw[W2ORDER[3]], 0)
         h_add(1)
         h_add(2)
+        copy_a(0, 0)
         h_leaky(1)
         qw2(1, w2b)
         flush()
         h_leaky(2)
         h_add(3)
+        copy_a(0, 1)
         qw2(2, w2c_)
         qw2(3, w2d_)
         emit_ready(3)
@@ -421,7 +475,9 @@ def tile_nonlocalmp_pa_kernel(tc, F, W1, b1, W2, b2, out):
                 add_b1(q - QB)
             if q in (QA, QA + 1):
                 stage1_a(1, q - QA)
-            h_add(q)
+                copy_a(1, q - QA)
+            if q not in G_TILES:
+                h_add(q)
             if q in (14, 15):
                 free_banks.append(a_bank[(0, q - 14)])
             emit_ready(q)

@@ -23,11 +23,11 @@ SLOPE = 0.2
 FLOPS = 2 * ROWS * C * 2 * C + 2 * ROWS * NODES * C * C
 
 SEQ = [(n, g) for n in range(UNITS) for g in range(2)]
-VSHARE = 84
-V_LEAKY = [12, 13, 14, 15]
-G_TILES = [9, 14, 19, 24, 29]
-G_PIECES = [[(0, 0, 4)], [(0, 4, 8)], [(1, 0, 4)], [(1, 4, 8)]]
-G_LEAD = 5
+VSHARE = 128
+V_LEAKY = [11, 12, 13, 14, 15]
+G_TILES = [7, 11, 15, 19, 23, 27, 31]
+G_PIECES = [[(0, 0, 6)], [(0, 6, 8), (1, 0, 3)], [(1, 3, 8)]]
+G_LEAD = 4
 U_SLOTS = 7
 H_SLOTS = 8
 QA = 12
@@ -136,6 +136,26 @@ def tile_nonlocalmp_pa_kernel(tc, F, W1, b1, W2, b2, out):
                 nc.vector.tensor_copy(out=dst[:, 0:vshare], in_=src[:, 0:vshare])
             if vshare < 128:
                 nc.scalar.copy(out=dst[:, vshare:128], in_=src[:, vshare:128])
+            return gq
+
+        def w1_cols(raw, t):
+            return raw[:].rearrange("p j (m t) -> p t m j", t=4)[:, t]
+
+        def w2_cols(raw, t):
+            return raw[:].rearrange("p j (t m) -> p t m j", t=4)[:, t]
+
+        def regroup_pe(raw, cols):
+            gq = grpp.tile([P, 512, 4], BF16, name="gq", align_bytes=64)
+            flat = gq[:].rearrange("p w j -> p (w j)")
+            for half in range(2):
+                ps = bank([P, 2, P, 4], BF16)[1]
+                for u in range(2):
+                    nc.tensor.matmul(
+                        out=ps[:, u], lhsT=identb[:], rhs=cols(raw, 2 * half + u), start=True, stop=True
+                    )
+                nc.scalar.copy(
+                    out=flat[:, half * 1024 : (half + 1) * 1024], in_=ps[:].rearrange("p u m j -> p (u m j)")
+                )
             return gq
 
         def quant(gq, codes, scales):
@@ -441,7 +461,7 @@ def tile_nonlocalmp_pa_kernel(tc, F, W1, b1, W2, b2, out):
         h_add(0)
         w1q(1, 0, g10)
         stage1_a(0, 1)
-        g13 = regroup_w1(w1raw[(1, 1, 1)], 128)
+        g13 = regroup_w1(w1raw[(1, 1, 1)], 0)
         w2a = regroup(w2raw[W2ORDER[0]], 0)
         h_leaky(0)
         w1q(1, 3, g13)
@@ -454,8 +474,8 @@ def tile_nonlocalmp_pa_kernel(tc, F, W1, b1, W2, b2, out):
         for g in range(2):
             stage1_b(1, g)
             nc.scalar.copy(out=b4[:, 1, g], in_=bps[(1, g)][:].rearrange("p t (b j) -> p j b t", j=NODES))
-        w2c_ = regroup(w2raw[W2ORDER[2]], 0)
-        w2d_ = regroup(w2raw[W2ORDER[3]], 0)
+        w2c_ = regroup_pe(w2raw[W2ORDER[2]], w2_cols)
+        w2d_ = regroup_pe(w2raw[W2ORDER[3]], w2_cols)
         h_add(1)
         h_add(2)
         copy_a(0, 0)

@@ -101,13 +101,14 @@ def tile_nonlocalmp_pa_kernel(tc, F, W1, b1, W2, b2, out):
 
         load_w1(0, 0, 0)
         load_w1(0, 0, 1)
+        load_w1(0, 1, 0)
         nc.sync.dma_start(out=fsb[:], in_=f_flat.rearrange("(f p) c -> p f c", p=P))
         nc.sync.dma_start(out=bt[0:8, :], in_=b2.rearrange("(r c) -> r c", c=P))
         nc.sync.dma_start(out=b1c[:], in_=b1.rearrange("(g p t) -> p g t", g=2, t=4))
         for g in range(2):
             for ab in range(2):
                 for kp in range(2):
-                    if (g, ab, kp) not in ((0, 0, 0), (0, 0, 1)):
+                    if (g, ab, kp) not in ((0, 0, 0), (0, 0, 1), (0, 1, 0)):
                         load_w1(g, ab, kp)
         for ch in range(2):
             for g in range(2):
@@ -432,24 +433,24 @@ def tile_nonlocalmp_pa_kernel(tc, F, W1, b1, W2, b2, out):
             nc.scalar.copy(out=fg32[:, kp], in_=xt[:].rearrange("p u c -> p c u"))
         btp = bank([P, P], BF16)[1]
         nc.tensor.transpose(btp[:], bt[:], identb[:])
+        nc.scalar.mul(out=b2r[:], in_=btp[:, 0:8], mul=1.0 - SLOPE)
+        nc.scalar.copy(out=b2v[:], in_=btp[:, 0:8])
+        for f in range(2):
+            plain = len([n for n in range(8 * f, 8 * f + 8) if n not in V_LEAKY])
+            nc.scalar.mul(out=b2l[f][:], in_=btp[:, 0:8], mul=SLOPE * plain)
 
         g01 = regroup_w1(w1raw[(0, 0, 1)], VSHARE)
-        w1q(0, 0, g00)
         g02 = regroup_w1(w1raw[(0, 1, 0)], VSHARE)
+        w1q(0, 0, g00)
+        w1q(0, 1, g01)
+        g03 = regroup_w1(w1raw[(0, 1, 1)], VSHARE)
         nc.vector.quantize_mx(
             out=fc[:].rearrange("p k c -> p (k c)").bitcast(FP8X4),
             scales=fs[:].rearrange("p k c -> p (k c)"),
             in_=fg[:].rearrange("p k c t -> p (k c t)"),
         )
-        w1q(0, 1, g01)
         stage1_a(0, 0)
-        g03 = regroup_w1(w1raw[(0, 1, 1)], VSHARE)
         w1q(0, 2, g02)
-        nc.vector.tensor_scalar_mul(out=b2r[:], in0=btp[:, 0:8], scalar1=1.0 - SLOPE)
-        nc.vector.tensor_copy(out=b2v[:], in_=btp[:, 0:8])
-        for f in range(2):
-            plain = len([n for n in range(8 * f, 8 * f + 8) if n not in V_LEAKY])
-            nc.vector.tensor_scalar_mul(out=b2l[f][:], in0=btp[:, 0:8], scalar1=SLOPE * plain)
         w1q(0, 3, g03)
         stage1_b(0, 0)
 

from contextlib import ExitStack

import concourse.bass as bass
import concourse.mybir as mybir
import concourse.tile as tile
from concourse.masks import make_identity

F32 = mybir.dt.float32
BF16 = mybir.dt.bfloat16
U32 = mybir.dt.uint32
U8 = mybir.dt.uint8
FP8X4 = mybir.dt.float8_e4m3fn_x4
ALU = mybir.AluOpType
ACT = mybir.ActivationFunctionType

P = 128
C = 1024
ROWS = 256
NODES = 16
HSETS = 8
UNITS = 16
SLOPE = 0.2
FLOPS = 2 * ROWS * C * 2 * C + 2 * ROWS * NODES * C * C

SEQ = [(n, g) for n in range(UNITS) for g in range(2)]
VSHARE = 128
V_LEAKY = [11, 12, 13, 14, 15]
G_TILES = [7, 11, 15, 19, 23, 27, 31]
G_PIECES = [[(0, 0, 6)], [(0, 6, 8), (1, 0, 3)], [(1, 3, 8)]]
G_LEAD = 4
U_SLOTS = 7
H_SLOTS = 8
QA = 12
DELAY = 7
GROUP = 4
QB = 10


def tile_nonlocalmp_pa_kernel(tc, F, W1, b1, W2, b2, out):
    nc = tc.nc
    f_flat = F.flatten_outer_dims()
    out_flat = out.flatten_outer_dims()

    with ExitStack() as ctx:
        const = ctx.enter_context(tc.tile_pool(name="const", bufs=1))
        rawp = ctx.enter_context(tc.tile_pool(name="rawp", bufs=8))
        grpp = ctx.enter_context(tc.tile_pool(name="grpp", bufs=4))
        up = ctx.enter_context(tc.tile_pool(name="up", bufs=1))
        hqp = ctx.enter_context(tc.tile_pool(name="hqp", bufs=H_SLOTS))
        hbp = ctx.enter_context(tc.tile_pool(name="hbp", bufs=4))
        rlp = ctx.enter_context(tc.tile_pool(name="rlp", bufs=16))
        resp = ctx.enter_context(tc.tile_pool(name="resp", bufs=4))
        bankp = ctx.enter_context(tc.psum_pool(name="bankp", bufs=1))
        sump = ctx.enter_context(tc.psum_pool(name="sump", bufs=1))
        ctx.enter_context(tc.manual_schedule())

        free_banks = ["w%d" % b for b in range(6)]
        a_bank = {}

        def bank(shape, dtype, keep=False):
            tag = free_banks[0]
            free_banks.remove(tag)
            if not keep:
                free_banks.append(tag)
            return tag, bankp.tile(shape, dtype, name=tag)

        ident32 = const.tile([P, P], F32, name="ident32")
        make_identity(nc, ident32[:])
        identb = const.tile([P, P], BF16, name="identb")
        make_identity(nc, identb[:])
        bt = const.tile([P, P], BF16, name="bt")
        nc.vector.memset(bt[:], 0.0)

        fsb = const.tile([P, 2, C], BF16, name="fsb")
        fg = const.tile([P, 2, ROWS, 4], BF16, name="fg", align_bytes=64)
        fc = const.tile([P, 2, ROWS], U32, name="fc", align_bytes=64)
        fs = const.tile([P, 2, ROWS], U8, name="fs", align_bytes=64)
        w1c = const.tile([P, 2, 2, 2, 512], U32, name="w1c", align_bytes=64)
        w1s = const.tile([P, 2, 2, 2, 512], U8, name="w1s", align_bytes=64)
        w2c = const.tile([P, 2, C], U32, name="w2c", align_bytes=64)
        w2s = const.tile([P, 2, C], U8, name="w2s", align_bytes=64)
        hcode = {}
        a4 = const.tile([P, 2, 2, HSETS, NODES, 4], F32, name="a4")
        b4 = const.tile([P, 2, 2, NODES, HSETS, 4], F32, name="b4")
        b1c = const.tile([P, 2, 4], BF16, name="b1c")
        b2r = const.tile([P, 8], F32, name="b2r")
        b2v = const.tile([P, 8], F32, name="b2v")
        b2l = [const.tile([P, 8], F32, name="b2l%d" % f) for f in range(2)]

        w1raw = {}
        w2raw = {}

        def load_w1(g, ab, kp):
            raw = rawp.tile([P, 4, 512], BF16, name="raw")
            r0 = ab * C + kp * 512
            nc.sync.dma_start(
                out=raw[:],
                in_=W1[r0 : r0 + 512, g * 512 : (g + 1) * 512].rearrange("(p j) w -> p j w", j=4),
            )
            w1raw[(g, ab, kp)] = raw

        load_w1(0, 0, 0)
        load_w1(0, 0, 1)
        load_w1(0, 1, 0)
        nc.sync.dma_start(out=fsb[:], in_=f_flat.rearrange("(f p) c -> p f c", p=P))
        nc.sync.dma_start(out=bt[0:8, :], in_=b2.rearrange("(r c) -> r c", c=P))
        nc.sync.dma_start(out=b1c[:], in_=b1.rearrange("(g p t) -> p g t", g=2, t=4))
        for g in range(2):
            for ab in range(2):
                for kp in range(2):
                    if (g, ab, kp) not in ((0, 0, 0), (0, 0, 1), (0, 1, 0)):
                        load_w1(g, ab, kp)
        for ch in range(2):
            for g in range(2):
                raw = rawp.tile([P, 4, 512], BF16, name="raw")
                nc.sync.dma_start(
                    out=raw[:],
                    in_=W2[g * 512 : (g + 1) * 512, ch * 512 : (ch + 1) * 512].rearrange("(p j) n -> p j n", j=4),
                )
                w2raw[(g, ch)] = raw

        def regroup(raw, vshare):
            gq = grpp.tile([P, 512, 4], BF16, name="gq", align_bytes=64)
            dst = gq[:].rearrange("p (c i) t -> p c t i", i=4)
            src = raw[:].rearrange("p t (c i) -> p c t i", i=4)
            if vshare > 0:
                nc.vector.tensor_copy(out=dst[:, 0:vshare], in_=src[:, 0:vshare])
            if vshare < 128:
                nc.scalar.copy(out=dst[:, vshare:128], in_=src[:, vshare:128])
            return gq

        def regroup_w1(raw, vshare):
            gq = grpp.tile([P, 512, 4], BF16, name="gq", align_bytes=64)
            dst = gq[:].rearrange("p (t m) j -> p m j t", t=4)
            src = raw[:].rearrange("p j (m t) -> p m j t", t=4)
            if vshare > 0:
                nc.vector.tensor_copy(out=dst[:, 0:vshare], in_=src[:, 0:vshare])
            if vshare < 128:
                nc.scalar.copy(out=dst[:, vshare:128], in_=src[:, vshare:128])
            return gq

        def w1_cols(raw, t):
            return raw[:].rearrange("p j (m t) -> p t m j", t=4)[:, t]

        def w2_cols(raw, t):
            return raw[:].rearrange("p j (t m) -> p t m j", t=4)[:, t]

        def regroup_pe(raw, cols):
            gq = grpp.tile([P, 512, 4], BF16, name="gq", align_bytes=64)
            flat = gq[:].rearrange("p w j -> p (w j)")
            for half in range(2):
                ps = bank([P, 2, P, 4], BF16)[1]
                for u in range(2):
                    nc.tensor.matmul(
                        out=ps[:, u], lhsT=identb[:], rhs=cols(raw, 2 * half + u), start=True, stop=True
                    )
                nc.scalar.copy(
                    out=flat[:, half * 1024 : (half + 1) * 1024], in_=ps[:].rearrange("p u m j -> p (u m j)")
                )
            return gq

        def quant(gq, codes, scales):
            nc.vector.quantize_mx(
                out=codes.bitcast(FP8X4), scales=scales, in_=gq[:].rearrange("p w t -> p (w t)")
            )

        def w1q(g, idx, gq):
            quant(gq, w1c[:, g, idx // 2, idx % 2, :], w1s[:, g, idx // 2, idx % 2, :])

        def stage1_pe(ps, g, ab, f):
            for t in range(4):
                for kp in range(2):
                    nc.tensor.matmul_mx(
                        out=ps[:, t, :],
                        lhsT=w1c[:, g, ab, kp, t * P : (t + 1) * P].bitcast(FP8X4),
                        lhsT_scale=w1s[:, g, ab, kp, t * P : (t + 1) * P],
                        rhs=fc[:, kp, f * P : (f + 1) * P].bitcast(FP8X4),
                        rhs_scale=fs[:, kp, f * P : (f + 1) * P],
                        start=(kp == 0),
                        stop=(kp == 1),
                    )

        aps = {}
        bps = {}

        def stage1_a(f, g):
            a_bank[(f, g)], ps = bank([P, 4, P], F32, True)
            stage1_pe(ps, g, 0, f)
            aps[(f, g)] = ps

        def stage1_b(f, g):
            ps = bank([P, 4, P], F32)[1]
            stage1_pe(ps, g, 1, f)
            bps[(f, g)] = ps

        def copy_a(f, g):
            nc.scalar.copy(out=a4[:, f, g], in_=aps[(f, g)][:].rearrange("p t (b i) -> p b i t", i=NODES))

        def evac_b(f, g):
            nc.vector.tensor_tensor(
                out=b4[:, f, g],
                in0=bps[(f, g)][:].rearrange("p t (b j) -> p j b t", j=NODES),
                in1=b1c[:, g, :].unsqueeze(1).unsqueeze(1).to_broadcast([P, NODES, HSETS, 4]),
                op=ALU.add,
            )

        def add_b1(g):
            nc.vector.tensor_tensor(
                out=b4[:, 1, g],
                in0=b4[:, 1, g],
                in1=b1c[:, g, :].unsqueeze(1).unsqueeze(1).to_broadcast([P, NODES, HSETS, 4]),
                op=ALU.add,
            )

        total = {}
        u_free = ["u%d" % b for b in range(U_SLOTS)]
        u_tag = {}
        gpieces = {}
        g_todo = [(q, piece) for q in G_TILES for piece in G_PIECES]
        banks = [(n, k) for n in range(UNITS) for k in range(4)]
        groups = []
        while banks:
            groups.append(banks[0:GROUP])
            banks = banks[GROUP:]
        to_sum = []
        to_leaky = []
        pending = []
        ready = []
        tcount = {}
        utile = {}
        hbt = {}
        rlt = {}
        done_g = {}

        def main_and_leaky(n, k):
            y = bank([P, 2, ROWS], F32)[1]
            for mloc in range(2):
                m = 2 * k + mloc
                for g in range(2):
                    nc.tensor.matmul_mx(
                        out=y[:, mloc, :],
                        lhsT=w2c[:, g, m * P : (m + 1) * P].bitcast(FP8X4),
                        lhsT_scale=w2s[:, g, m * P : (m + 1) * P],
                        rhs=hcode[n][0][:, g, :].bitcast(FP8X4),
                        rhs_scale=hcode[n][1][:, g, :],
                        start=(g == 0),
                        stop=(g == 1),
                    )
            rl = rlp.tile([P, 2, 2, ROWS], F32, name="rl")
            rlt[(n, k)] = rl
            for mloc in range(2):
                m = 2 * k + mloc
                if n in V_LEAKY:
                    nc.scalar.activation(
                        out=rl[:, 0, mloc, :], in_=y[:, mloc, :], func=ACT.Identity, bias=b2v[:, m : m + 1], scale=1.0
                    )
                else:
                    nc.scalar.activation(
                        out=rl[:, 0, mloc, :], in_=y[:, mloc, :], func=ACT.Relu, bias=b2r[:, m : m + 1], scale=1.0 - SLOPE
                    )
            if n in V_LEAKY:
                return
            if n % 8 == 0:
                for mloc in range(2):
                    m = 2 * k + mloc
                    nc.scalar.activation(
                        out=rl[:, 1, mloc, :], in_=y[:, mloc, :], func=ACT.Identity, bias=b2l[n // 8][:, m : m + 1], scale=SLOPE
                    )
            else:
                nc.scalar.mul(out=rl[:, 1], in_=y[:], mul=SLOPE)

        def v_leaky(n, k):
            rl = rlt[(n, k)]
            nc.vector.scalar_tensor_tensor(
                out=rl[:, 1], in0=rl[:, 0], scalar=SLOPE, in1=rl[:, 0], op0=ALU.mult, op1=ALU.max
            )

        def finish(f, ch):
            res = resp.tile([P, 512], F32, name="res")
            if f == 1:
                nc.vector.tensor_copy(out=res[:], in_=total[(f, ch)][:])
            else:
                nc.scalar.copy(out=res[:], in_=total[(f, ch)][:])
            nc.sync.dma_start(
                out=out_flat[f * P : (f + 1) * P, ch * 512 : (ch + 1) * 512], in_=res[:]
            )

        def sum_transposes(n, k):
            f, ch = n // 8, k // 2
            terms = 0
            for v in range(8):
                terms = terms + (1 if 8 * f + v in V_LEAKY else 2)
            if (f, ch) not in total:
                total[(f, ch)] = sump.tile([P, 512], F32, name="tot%d" % ch)
            for m in (2 * k, 2 * k + 1):
                mm = m % 4
                for j2 in range(2):
                    for term in ([1] if n in V_LEAKY else [0, 1]):
                        cnt = tcount.get((f, ch), 0)
                        tcount[(f, ch)] = cnt + 1
                        nc.tensor.matmul(
                            out=total[(f, ch)][:, mm * P : (mm + 1) * P],
                            lhsT=rlt[(n, k)][:, term, m % 2, j2 * P : (j2 + 1) * P],
                            rhs=ident32[:],
                            is_transpose=True,
                            start=(cnt == 0),
                            stop=(cnt == 8 * terms - 1),
                        )
            if tcount[(f, ch)] == 8 * terms:
                finish(f, ch)

        def leaky_due(q):
            while to_leaky and 2 * to_leaky[0][0] + DELAY + to_leaky[0][1] // 2 <= q:
                n, k = to_leaky[0]
                to_leaky.remove((n, k))
                v_leaky(n, k)

        def run_group(group, q):
            for n, k in group:
                main_and_leaky(n, k)
                if n in V_LEAKY:
                    to_leaky.append((n, k))
            leaky_due(q)
            for n, k in list(to_sum):
                if (n, k) not in to_leaky:
                    to_sum.remove((n, k))
                    sum_transposes(n, k)
            to_sum.extend(group)

        def flush():
            while pending:
                q = pending[0]
                pending.remove(q)
                n, g = SEQ[q]
                if n not in hcode:
                    hcode[n] = (
                        hqp.tile([P, 2, ROWS], U32, name="hc", align_bytes=64),
                        hqp.tile([P, 2, ROWS], U8, name="hs", align_bytes=64),
                    )
                nc.vector.quantize_mx(
                    out=hcode[n][0][:, g, :].bitcast(FP8X4), scales=hcode[n][1][:, g, :], in_=hbt[q][:]
                )
                done_g[n] = done_g.get(n, 0) + 1
                if done_g[n] == 2:
                    ready.append(n)

        def emit_ready(q):
            while groups and groups[0][-1][0] in ready:
                group = groups[0]
                groups.remove(group)
                run_group(group, q)

        def h_add(q):
            n, g = SEQ[q]
            f, jp = n // 8, n % 8
            tag = u_free[0]
            u_free.remove(tag)
            u_tag[q] = tag
            u = up.tile([P, 2, HSETS, NODES, 4], F32, name=tag)
            utile[q] = u
            nc.vector.tensor_tensor(
                out=u[:],
                in0=aps[(f, g)][:]
                .rearrange("p t (b i) -> p b i t", i=NODES)
                .unsqueeze(1)
                .to_broadcast([P, 2, HSETS, NODES, 4]),
                in1=b4[:, f, g, 2 * jp : 2 * jp + 2].unsqueeze(3).to_broadcast([P, 2, HSETS, NODES, 4]),
                op=ALU.add,
            )
            flush()

        def leaky_piece(dst, src):
            nc.vector.scalar_tensor_tensor(out=dst, in0=src, scalar=SLOPE, in1=src, op0=ALU.mult, op1=ALU.max)

        def g_piece(tag):
            q, piece = g_todo[0]
            g_todo.remove((q, piece))
            n, g = SEQ[q]
            f, jp = n // 8, n % 8
            ug = up.tile([P, sum([b1 - b0 for jj, b0, b1 in piece]), NODES, 4], F32, name=tag)
            gpieces.setdefault(q, []).append((ug, tag, sum([b1 - b0 for jj, b0, b1 in piece]) * NODES * 4))
            at = 0
            for jj, b0, b1 in piece:
                nc.gpsimd.tensor_tensor(
                    out=ug[:, at : at + b1 - b0],
                    in0=a4[:, f, g, b0:b1],
                    in1=b4[:, f, g, 2 * jp + jj, b0:b1].unsqueeze(2).to_broadcast([P, b1 - b0, NODES, 4]),
                    op=ALU.add,
                )
                at = at + b1 - b0

        def release(tag, q):
            if g_todo and g_todo[0][0] - G_LEAD <= q:
                g_piece(tag)
            else:
                u_free.append(tag)

        def h_leaky(q):
            hb16 = hbp.tile([P, 4 * ROWS], BF16, name="hb16", align_bytes=64)
            hbt[q] = hb16
            pending.append(q)
            if q in G_TILES:
                at = 0
                for ug, tag, size in gpieces[q]:
                    leaky_piece(hb16[:, at : at + size], ug[:].rearrange("p b i t -> p (b i t)"))
                    at = at + size
                for ug, tag, size in gpieces[q][0:-1]:
                    u_free.append(tag)
                release(gpieces[q][-1][1], q)
                return
            leaky_piece(hb16[:], utile[q][:].rearrange("p j b i t -> p (j b i t)"))
            release(u_tag[q], q)

        W2ORDER = [(0, 0), (1, 0), (0, 1), (1, 1)]

        def qw2(idx, gq):
            gg, ch = W2ORDER[idx]
            quant(gq, w2c[:, gg, ch * 512 : (ch + 1) * 512], w2s[:, gg, ch * 512 : (ch + 1) * 512])

        g00 = regroup_w1(w1raw[(0, 0, 0)], VSHARE)

        fsb32 = fsb[:].bitcast(F32)
        fg32 = fg[:].bitcast(F32)
        for kp in range(2):
            xt = bank([P, 2, ROWS], F32)[1]
            for f in range(2):
                for u in range(2):
                    nc.tensor.transpose(
                        xt[:, u, f * P : (f + 1) * P],
                        fsb32[:, f, kp * 256 + u : (kp + 1) * 256 : 2],
                        ident32[:],
                    )
            nc.scalar.copy(out=fg32[:, kp], in_=xt[:].rearrange("p u c -> p c u"))
        btp = bank([P, P], BF16)[1]
        nc.tensor.transpose(btp[:], bt[:], identb[:])
        nc.scalar.mul(out=b2r[:], in_=btp[:, 0:8], mul=1.0 - SLOPE)
        nc.scalar.copy(out=b2v[:], in_=btp[:, 0:8])
        for f in range(2):
            plain = len([n for n in range(8 * f, 8 * f + 8) if n not in V_LEAKY])
            nc.scalar.mul(out=b2l[f][:], in_=btp[:, 0:8], mul=SLOPE * plain)

        g01 = regroup_w1(w1raw[(0, 0, 1)], VSHARE)
        g02 = regroup_w1(w1raw[(0, 1, 0)], VSHARE)
        w1q(0, 0, g00)
        w1q(0, 1, g01)
        g03 = regroup_w1(w1raw[(0, 1, 1)], VSHARE)
        nc.vector.quantize_mx(
            out=fc[:].rearrange("p k c -> p (k c)").bitcast(FP8X4),
            scales=fs[:].rearrange("p k c -> p (k c)"),
            in_=fg[:].rearrange("p k c t -> p (k c t)"),
        )
        stage1_a(0, 0)
        w1q(0, 2, g02)
        w1q(0, 3, g03)
        stage1_b(0, 0)

        g10 = regroup_w1(w1raw[(1, 0, 0)], 0)
        g11 = regroup_w1(w1raw[(1, 0, 1)], 128)
        evac_b(0, 0)
        g12 = regroup_w1(w1raw[(1, 1, 0)], 0)
        w1q(1, 1, g11)
        h_add(0)
        w1q(1, 0, g10)
        stage1_a(0, 1)
        g13 = regroup_w1(w1raw[(1, 1, 1)], 0)
        w2a = regroup(w2raw[W2ORDER[0]], 0)
        h_leaky(0)
        w1q(1, 3, g13)
        w1q(1, 2, g12)
        stage1_b(0, 1)
        w2b = regroup(w2raw[W2ORDER[1]], 0)
        flush()
        qw2(0, w2a)
        evac_b(0, 1)
        for g in range(2):
            stage1_b(1, g)
            nc.scalar.copy(out=b4[:, 1, g], in_=bps[(1, g)][:].rearrange("p t (b j) -> p j b t", j=NODES))
        w2c_ = regroup_pe(w2raw[W2ORDER[2]], w2_cols)
        w2d_ = regroup_pe(w2raw[W2ORDER[3]], w2_cols)
        h_add(1)
        h_add(2)
        copy_a(0, 0)
        h_leaky(1)
        qw2(1, w2b)
        flush()
        h_leaky(2)
        h_add(3)
        copy_a(0, 1)
        qw2(2, w2c_)
        qw2(3, w2d_)
        emit_ready(3)
        h_leaky(3)
        emit_ready(3)
        for q in range(4, len(SEQ)):
            if q in (QB, QB + 1):
                add_b1(q - QB)
            if q in (QA, QA + 1):
                stage1_a(1, q - QA)
                copy_a(1, q - QA)
            if q not in G_TILES:
                h_add(q)
            if q in (14, 15):
                free_banks.append(a_bank[(0, q - 14)])
            emit_ready(q)
            h_leaky(q)
            leaky_due(q)
        flush()
        emit_ready(3 * len(SEQ))
        leaky_due(3 * len(SEQ))
        for n, k in to_sum:
            sum_transposes(n, k)
